import numpy as np
import ml_dtypes


def mxq(x, axis, fmt="e4m3"):
    dtype, down = {"e4m3": (ml_dtypes.float8_e4m3fn, 7), "e5m2": (ml_dtypes.float8_e5m2, 14)}[fmt]
    v = np.moveaxis(np.asarray(x, np.float32).astype(ml_dtypes.bfloat16).astype(np.float64), axis, -1)
    blocks = v.reshape(v.shape[:-1] + (-1, 32))
    amax = np.abs(blocks).max(-1, keepdims=True)
    byte = np.maximum(np.where(amax > 0, np.frexp(amax)[1] - 1 + 127, 0) - down, 1)
    scale = np.exp2(byte - 127.0)
    codes = (blocks / scale).astype(np.float32).astype(dtype).astype(np.float64)
    return np.moveaxis((codes * scale).reshape(v.shape), -1, axis)


WIDE = False


def mx_kscale(k):
    if not WIDE:
        return np.ones(k)
    levels = np.array([10, -10, 5, -5, 0])
    a = np.random.permutation(np.resize(levels, k // 512 * 4)).reshape(k // 512, 4)
    idx = np.arange(k)
    return np.exp2(a[idx // 512, idx % 128 // 32])


BF16 = ml_dtypes.bfloat16


def bf(x):
    return np.asarray(x, np.float32).astype(BF16)


def f64(x):
    return np.asarray(x).astype(np.float64)


E2M1 = np.array([0.0, 0.5, 1.0, 1.5, 2.0, 3.0, 4.0, 6.0, -0.0, -0.5, -1.0, -1.5, -2.0, -3.0, -4.0, -6.0])


def pack_weight(w, fmt):
    k, n = w.shape
    w = f64(bf(w)).reshape(k // 32, 32, n)
    amax = np.abs(w).max(1)
    if fmt == "e4m3":
        byte = np.frexp(amax)[1] - 1 + 127 - 7
    else:
        mant, ex = np.frexp(amax / 6.0)
        byte = np.where(mant > 0.5, ex, ex - 1) + 127
    byte = np.clip(np.where(amax > 0, byte, 1), 1, 254)
    scaled = (w * np.exp2(127.0 - byte)[:, None, :]).reshape(k, n).astype(np.float32)
    by_word = np.ascontiguousarray(scaled.reshape(k // 512, 128, 4, n).transpose(0, 1, 3, 2))
    if fmt == "e4m3":
        words = by_word.astype(ml_dtypes.float8_e4m3fn).view(np.uint8)
    else:
        c = by_word.astype(ml_dtypes.float4_e2m1fn).view(np.uint8) & 0xF
        words = c[..., 0::2] | (c[..., 1::2] << 4)
    return np.ascontiguousarray(words), np.ascontiguousarray(byte.astype(np.uint8).reshape(k // 512, 16, n))


def unpack_weight(words, scales, fmt):
    g, p, n, _ = words.shape
    if fmt == "e4m3":
        vals = np.ascontiguousarray(words).view(ml_dtypes.float8_e4m3fn).astype(np.float64)
    else:
        nib = np.empty((g, p, n, 4), np.uint8)
        nib[..., 0::2] = words & 0xF
        nib[..., 1::2] = words >> 4
        vals = E2M1[nib]
    vals = vals * np.repeat(np.exp2(scales.astype(np.float64) - 127.0), 8, axis=1)[..., None]
    return vals.transpose(0, 1, 3, 2).reshape(g * 512, n)

def pack4(w):
    words, scales = pack_weight(w, "e2m1")
    return words.reshape(words.shape[0], 128, -1), scales


def unpack4(words, scales):
    return unpack_weight(words.reshape(words.shape[0], 128, -1, 2), scales, "e2m1")


B, S, D = 4, 1024, 512
ROPE_BASE = 10000.0


def rope_tables():
    inv_freq = 1.0 / ROPE_BASE ** (np.arange(0, D, 2) / D)
    freqs = np.outer(np.arange(S), inv_freq)
    emb = np.concatenate([freqs, freqs], axis=-1)
    return np.cos(emb), np.sin(emb)


def rotate_half(u):
    u1, u2 = np.split(u, 2, axis=-1)
    return np.concatenate([-u2, u1], axis=-1)


def setup_inputs():
    s = mx_kscale(D)
    c, sn = rope_tables()
    w = 1.0 / np.sqrt(D)
    x = bf(np.random.standard_normal((B, S, D)) * s)
    wq = np.random.standard_normal((D, D)) * w / s[None, :]
    wk = np.random.standard_normal((D, D)) * w / s[None, :]
    wq_words, wq_scales = pack4(np.ascontiguousarray(wq.T))
    wk_words, wk_scales = pack4(np.ascontiguousarray(wk.T))
    return {"x": x,
            "cos": bf(c),
            "sin": bf(sn),
            "Wq_words": wq_words,
            "Wq_scales": wq_scales,
            "Wk_words": wk_words,
            "Wk_scales": wk_scales}


def reference(x, cos, sin, Wq_words, Wq_scales, Wk_words, Wk_scales):
    xq = mxq(f64(x), 2, "e4m3")
    q = xq @ unpack4(Wq_words, Wq_scales)
    k = xq @ unpack4(Wk_words, Wk_scales)
    c, sn = f64(cos), f64(sin)
    q_rot = q * c + rotate_half(q) * sn
    k_rot = k * c + rotate_half(k) * sn
    return q_rot, k_rot

@@ -1,0 +1,146 @@
+import concourse.mybir as mybir
+from concourse.masks import make_identity
+
+F32 = mybir.dt.float32
+BF16 = mybir.dt.bfloat16
+U8 = mybir.dt.uint8
+U32 = mybir.dt.uint32
+I32 = mybir.dt.int32
+FP8X4 = mybir.dt.float8_e4m3fn_x4
+FP4X4 = mybir.dt.float4_e2m1fn_x4
+ALU = mybir.AluOpType
+
+P = 128
+BATCH = 4
+SEQ = 1024
+DIM = 512
+HALF = DIM // 2
+WORDS = DIM // 2
+PACK = 4
+ROWS = SEQ // P
+PAIR = 2
+WEIGHTS = 2
+
+FLOPS = 2 * BATCH * SEQ * DIM * WEIGHTS * DIM
+
+
+def load_weight(nc, words_dram, scales_dram, words, scales, w):
+    nc.sync.dma_start(
+        out=words[:, :, w, :].bitcast(I32),
+        in_=words_dram[0].bitcast(I32).rearrange("p (h c) -> p h c", h=2),
+    )
+    for quadrant in range(4):
+        nc.sync.dma_start(
+            out=scales[32 * quadrant : 32 * quadrant + 4, :, w, :].bitcast(I32),
+            in_=scales_dram[0, 4 * quadrant : 4 * quadrant + 4, :]
+            .bitcast(I32)
+            .rearrange("q (h c) -> q h c", h=2),
+        )
+
+
+def tile_attention_pa_t_kernel(
+    tc, x, cos, sin, wq_words, wq_scales, wk_words, wk_scales, out_q, out_k
+):
+    nc = tc.nc
+    outs = (out_q, out_k)
+    groups = [(b, j0) for b in range(BATCH) for j0 in range(0, ROWS, PAIR)]
+
+    with (
+        tc.tile_pool(name="keep", bufs=1) as keep,
+        tc.tile_pool(name="quant", bufs=3) as quant,
+        tc.tile_pool(name="rope", bufs=3) as rope,
+        tc.psum_pool(name="flip", bufs=2) as flip,
+        tc.psum_pool(name="sums", bufs=6) as sums,
+    ):
+        x_sb = keep.tile([P, BATCH, ROWS, DIM], BF16)
+        cos_sb = keep.tile([P, ROWS, DIM], BF16)
+        sin_sb = keep.tile([P, ROWS, DIM], BF16)
+        w_words = keep.tile([P, 2, WEIGHTS, 2 * HALF], U8, align_bytes=64)
+        w_scales = keep.tile([P, 2, WEIGHTS, HALF], U8, align_bytes=64)
+        ident = keep.tile([P, P], F32)
+
+        nc.vector.memset(w_scales[:].bitcast(I32), 0)
+        make_identity(nc, ident[:])
+
+        x_rows = [x[b].rearrange("(p j) d -> p j d", j=ROWS) for b in range(BATCH)]
+        cos_rows = cos.rearrange("(p j) d -> p j d", j=ROWS)
+        sin_rows = sin.rearrange("(p j) d -> p j d", j=ROWS)
+        for j0 in range(0, ROWS, PAIR):
+            piece = slice(j0, j0 + PAIR)
+            nc.sync.dma_start(out=x_sb[:, 0, piece, :], in_=x_rows[0][:, piece, :])
+            if j0 == 0:
+                load_weight(nc, wq_words, wq_scales, w_words, w_scales, 0)
+                load_weight(nc, wk_words, wk_scales, w_words, w_scales, 1)
+            nc.sync.dma_start(out=cos_sb[:, piece, :], in_=cos_rows[:, piece, :])
+            nc.sync.dma_start(out=sin_sb[:, piece, :], in_=sin_rows[:, piece, :])
+        for b in range(1, BATCH):
+            nc.sync.dma_start(out=x_sb[:, b], in_=x_rows[b])
+
+        def quantise(b, j0):
+            flipped = flip.tile([P, PAIR, 2, P], F32)
+            for a in range(PAIR):
+                x_words = x_sb[:, b, j0 + a, :].bitcast(F32)
+                for u in range(2):
+                    nc.tensor.transpose(flipped[:, a, u, :], x_words[:, u : WORDS : 2], ident[:])
+            grouped = quant.tile([P, PAIR * P * PACK], BF16, align_bytes=64)
+            nc.scalar.copy(
+                out=grouped[:].bitcast(F32).rearrange("p (a r u) -> p a r u", a=PAIR, u=2),
+                in_=flipped[:].rearrange("p a u r -> p a r u"),
+            )
+            x_codes = quant.tile([P, PAIR * P], U32, align_bytes=64)
+            x_scales = quant.tile([P, PAIR * P], U8, align_bytes=64)
+            nc.vector.quantize_mx(
+                out=x_codes[:].bitcast(FP8X4), scales=x_scales[:], in_=grouped[:]
+            )
+            return x_codes, x_scales
+
+        def project(x_codes, x_scales, a):
+            tokens = slice(a * P, (a + 1) * P)
+            banks = []
+            for h in range(2):
+                bank = sums.tile([P, WEIGHTS, HALF], F32, name="bank")
+                nc.tensor.matmul_mx(
+                    out=bank[:].rearrange("p w c -> p (w c)"),
+                    lhsT=x_codes[:, tokens].bitcast(FP8X4),
+                    lhsT_scale=x_scales[:, tokens],
+                    rhs=w_words[:, h].rearrange("p w c -> p (w c)").bitcast(FP4X4),
+                    rhs_scale=w_scales[:, h].rearrange("p w c -> p (w c)"),
+                    start=True,
+                    stop=True,
+                )
+                banks.append(bank)
+            return banks
+
+        def table(rows_sb, j, h):
+            half = rows_sb[:, j, h * HALF : (h + 1) * HALF]
+            return half.unsqueeze(1).to_broadcast([P, WEIGHTS, HALF])
+
+        def rotate_and_store(b, j0, x_codes, x_scales):
+            rot = rope.tile([P, WEIGHTS, PAIR, 2, HALF], F32)
+            crossed = rope.tile([P, WEIGHTS, PAIR, 2, HALF], F32)
+            for a in range(PAIR):
+                low, high = project(x_codes, x_scales, a)
+                j = j0 + a
+                nc.vector.tensor_tensor(rot[:, :, a, 0, :], low[:], table(cos_sb, j, 0), ALU.mult)
+                nc.vector.tensor_tensor(crossed[:, :, a, 1, :], low[:], table(sin_sb, j, 1), ALU.mult)
+                nc.vector.tensor_tensor(rot[:, :, a, 1, :], high[:], table(cos_sb, j, 1), ALU.mult)
+                nc.vector.tensor_tensor(crossed[:, :, a, 0, :], high[:], table(sin_sb, j, 0), ALU.mult)
+            rot_halves = rot[:].rearrange("p w a h c -> p (w a) h c")
+            crossed_halves = crossed[:].rearrange("p w a h c -> p (w a) h c")
+            for h, engine, op in ((0, nc.gpsimd, ALU.subtract), (1, nc.vector, ALU.add)):
+                engine.tensor_tensor(
+                    rot_halves[:, :, h, :], rot_halves[:, :, h, :], crossed_halves[:, :, h, :], op
+                )
+            for w in range(WEIGHTS):
+                out_rows = outs[w][b].rearrange("(p j) d -> p j d", j=ROWS)
+                nc.sync.dma_start(
+                    out=out_rows[:, j0 : j0 + PAIR, :],
+                    in_=rot[:, w].rearrange("p a h c -> p a (h c)"),
+                )
+
+        ready = quantise(*groups[0])
+        for g, (b, j0) in enumerate(groups):
+            x_codes, x_scales = ready
+            if g + 1 < len(groups):
+                ready = quantise(*groups[g + 1])
+            rotate_and_store(b, j0, x_codes, x_scales)

@@ -9,32 +9,30 @@ I32 = mybir.dt.int32
 FP8X4 = mybir.dt.float8_e4m3fn_x4
 FP4X4 = mybir.dt.float4_e2m1fn_x4
 ALU = mybir.AluOpType
+ACT = mybir.ActivationFunctionType
 
 P = 128
 BATCH = 4
 SEQ = 1024
 DIM = 512
-HALF = DIM // 2
 WORDS = DIM // 2
 PACK = 4
 ROWS = SEQ // P
-PAIR = 2
+CHUNKS = DIM // P
+TILES = 4
+UNIT = TILES * P
+SWEEPS = ROWS // TILES
 WEIGHTS = 2
 
 FLOPS = 2 * BATCH * SEQ * DIM * WEIGHTS * DIM
 
 
 def load_weight(nc, words_dram, scales_dram, words, scales, w):
-    nc.sync.dma_start(
-        out=words[:, :, w, :].bitcast(I32),
-        in_=words_dram[0].bitcast(I32).rearrange("p (h c) -> p h c", h=2),
-    )
+    nc.sync.dma_start(out=words[:, w, :].bitcast(I32), in_=words_dram[0].bitcast(I32))
     for quadrant in range(4):
         nc.sync.dma_start(
-            out=scales[32 * quadrant : 32 * quadrant + 4, :, w, :].bitcast(I32),
-            in_=scales_dram[0, 4 * quadrant : 4 * quadrant + 4, :]
-            .bitcast(I32)
-            .rearrange("q (h c) -> q h c", h=2),
+            out=scales[32 * quadrant : 32 * quadrant + 4, w, :].bitcast(I32),
+            in_=scales_dram[0, 4 * quadrant : 4 * quadrant + 4, :].bitcast(I32),
         )
 
 
@@ -43,104 +41,125 @@ def tile_attention_pa_t_kernel(
 ):
     nc = tc.nc
     outs = (out_q, out_k)
-    groups = [(b, j0) for b in range(BATCH) for j0 in range(0, ROWS, PAIR)]
 
     with (
         tc.tile_pool(name="keep", bufs=1) as keep,
-        tc.tile_pool(name="quant", bufs=3) as quant,
-        tc.tile_pool(name="rope", bufs=3) as rope,
+        tc.tile_pool(name="quant", bufs=2) as quant,
+        tc.tile_pool(name="prods", bufs=6) as prods,
+        tc.tile_pool(name="rows", bufs=3) as rows,
         tc.psum_pool(name="flip", bufs=2) as flip,
-        tc.psum_pool(name="sums", bufs=6) as sums,
+        tc.psum_pool(name="sums", bufs=4) as sums,
+        tc.psum_pool(name="back", bufs=2) as back,
     ):
         x_sb = keep.tile([P, BATCH, ROWS, DIM], BF16)
-        cos_sb = keep.tile([P, ROWS, DIM], BF16)
-        sin_sb = keep.tile([P, ROWS, DIM], BF16)
-        w_words = keep.tile([P, 2, WEIGHTS, 2 * HALF], U8, align_bytes=64)
-        w_scales = keep.tile([P, 2, WEIGHTS, HALF], U8, align_bytes=64)
+        raw = keep.tile([P, 2, ROWS, DIM], BF16)
+        tables = keep.tile([P, CHUNKS, 2, SEQ], BF16)
+        w_words = keep.tile([P, WEIGHTS, 2 * DIM], U8, align_bytes=64)
+        w_scales = keep.tile([P, WEIGHTS, DIM], U8, align_bytes=64)
         ident = keep.tile([P, P], F32)
+        ident_bf = keep.tile([P, P], BF16)
 
         nc.vector.memset(w_scales[:].bitcast(I32), 0)
         make_identity(nc, ident[:])
+        make_identity(nc, ident_bf[:])
 
         x_rows = [x[b].rearrange("(p j) d -> p j d", j=ROWS) for b in range(BATCH)]
-        cos_rows = cos.rearrange("(p j) d -> p j d", j=ROWS)
-        sin_rows = sin.rearrange("(p j) d -> p j d", j=ROWS)
-        for j0 in range(0, ROWS, PAIR):
-            piece = slice(j0, j0 + PAIR)
-            nc.sync.dma_start(out=x_sb[:, 0, piece, :], in_=x_rows[0][:, piece, :])
-            if j0 == 0:
-                load_weight(nc, wq_words, wq_scales, w_words, w_scales, 0)
-                load_weight(nc, wk_words, wk_scales, w_words, w_scales, 1)
-            nc.sync.dma_start(out=cos_sb[:, piece, :], in_=cos_rows[:, piece, :])
-            nc.sync.dma_start(out=sin_sb[:, piece, :], in_=sin_rows[:, piece, :])
-        for b in range(1, BATCH):
-            nc.sync.dma_start(out=x_sb[:, b], in_=x_rows[b])
+        table_rows = [t.rearrange("(p j) d -> p j d", j=ROWS) for t in (cos, sin)]
+        for s in range(SWEEPS):
+            piece = slice(s * TILES, (s + 1) * TILES)
+            for b in range(BATCH):
+                nc.sync.dma_start(out=x_sb[:, b, piece, :], in_=x_rows[b][:, piece, :])
+                if b == 0:
+                    if s == 0:
+                        load_weight(nc, wq_words, wq_scales, w_words, w_scales, 0)
+                        load_weight(nc, wk_words, wk_scales, w_words, w_scales, 1)
+                    for t in range(2):
+                        nc.sync.dma_start(out=raw[:, t, piece, :], in_=table_rows[t][:, piece, :])
 
-        def quantise(b, j0):
-            flipped = flip.tile([P, PAIR, 2, P], F32)
-            for a in range(PAIR):
-                x_words = x_sb[:, b, j0 + a, :].bitcast(F32)
-                for u in range(2):
-                    nc.tensor.transpose(flipped[:, a, u, :], x_words[:, u : WORDS : 2], ident[:])
-            grouped = quant.tile([P, PAIR * P * PACK], BF16, align_bytes=64)
-            nc.scalar.copy(
-                out=grouped[:].bitcast(F32).rearrange("p (a r u) -> p a r u", a=PAIR, u=2),
-                in_=flipped[:].rearrange("p a u r -> p a r u"),
-            )
-            x_codes = quant.tile([P, PAIR * P], U32, align_bytes=64)
-            x_scales = quant.tile([P, PAIR * P], U8, align_bytes=64)
-            nc.vector.quantize_mx(
-                out=x_codes[:].bitcast(FP8X4), scales=x_scales[:], in_=grouped[:]
-            )
+        def turn_tables(s):
+            for j in range(s * TILES, (s + 1) * TILES):
+                cols = slice(j * P, (j + 1) * P)
+                for t in range(2):
+                    turned = flip.tile([P, CHUNKS, P], BF16, name="flipped")
+                    for c in range(CHUNKS):
+                        nc.tensor.transpose(turned[:, c, :], raw[:, t, j, c * P : (c + 1) * P], ident_bf[:])
+                    if t == 0:
+                        engine_copy = nc.vector.tensor_copy if s == 0 else nc.scalar.copy
+                        engine_copy(out=tables[:, :, 0, cols], in_=turned[:])
+                    else:
+                        nc.scalar.copy(out=tables[:, 0:2, 1, cols], in_=turned[:, 2:4, :])
+                        nc.scalar.activation(
+                            out=tables[:, 2:4, 1, cols], in_=turned[:, 0:2, :], func=ACT.Copy, scale=-1.0
+                        )
+
+        def quantise(s, b):
+            grouped = quant.tile([P, UNIT * PACK], BF16, align_bytes=64)
+            for half in range(2):
+                flipped = flip.tile([P, 2, 2, P], F32, name="flipped")
+                for a in range(2):
+                    x_words = x_sb[:, b, s * TILES + 2 * half + a, :].bitcast(F32)
+                    for u in range(2):
+                        nc.tensor.transpose(flipped[:, a, u, :], x_words[:, u : WORDS : 2], ident[:])
+                nc.scalar.copy(
+                    out=grouped[:, half * 2 * P * PACK : (half + 1) * 2 * P * PACK]
+                    .bitcast(F32)
+                    .rearrange("p (a r u) -> p a r u", a=2, u=2),
+                    in_=flipped[:].rearrange("p a u r -> p a r u"),
+                )
+            x_codes = quant.tile([P, UNIT], U32, align_bytes=64)
+            x_scales = quant.tile([P, UNIT], U8, align_bytes=64)
+            nc.vector.quantize_mx(out=x_codes[:].bitcast(FP8X4), scales=x_scales[:], in_=grouped[:])
             return x_codes, x_scales
 
-        def project(x_codes, x_scales, a):
-            tokens = slice(a * P, (a + 1) * P)
-            banks = []
-            for h in range(2):
-                bank = sums.tile([P, WEIGHTS, HALF], F32, name="bank")
-                nc.tensor.matmul_mx(
-                    out=bank[:].rearrange("p w c -> p (w c)"),
-                    lhsT=x_codes[:, tokens].bitcast(FP8X4),
-                    lhsT_scale=x_scales[:, tokens],
-                    rhs=w_words[:, h].rearrange("p w c -> p (w c)").bitcast(FP4X4),
-                    rhs_scale=w_scales[:, h].rearrange("p w c -> p (w c)"),
-                    start=True,
-                    stop=True,
-                )
-                banks.append(bank)
-            return banks
+        def products(s, w, c, x_codes, x_scales):
+            bank = sums.tile([P, UNIT], F32, name="bank")
+            nc.tensor.matmul_mx(
+                out=bank[:],
+                lhsT=w_words[:, w, c * 2 * P : (c + 1) * 2 * P].bitcast(FP4X4),
+                lhsT_scale=w_scales[:, w, c * P : (c + 1) * P],
+                rhs=x_codes[:].bitcast(FP8X4),
+                rhs_scale=x_scales[:],
+                start=True,
+                stop=True,
+            )
+            prod = prods.tile([P, 2, UNIT], F32, name="prod")
+            nc.vector.tensor_tensor(
+                prod[:],
+                bank[:].unsqueeze(1).to_broadcast([P, 2, UNIT]),
+                tables[:, c, :, s * UNIT : (s + 1) * UNIT],
+                ALU.mult,
+            )
+            return prod
 
-        def table(rows_sb, j, h):
-            half = rows_sb[:, j, h * HALF : (h + 1) * HALF]
-            return half.unsqueeze(1).to_broadcast([P, WEIGHTS, HALF])
-
-        def rotate_and_store(b, j0, x_codes, x_scales):
-            rot = rope.tile([P, WEIGHTS, PAIR, 2, HALF], F32)
-            crossed = rope.tile([P, WEIGHTS, PAIR, 2, HALF], F32)
-            for a in range(PAIR):
-                low, high = project(x_codes, x_scales, a)
-                j = j0 + a
-                nc.vector.tensor_tensor(rot[:, :, a, 0, :], low[:], table(cos_sb, j, 0), ALU.mult)
-                nc.vector.tensor_tensor(crossed[:, :, a, 1, :], low[:], table(sin_sb, j, 1), ALU.mult)
-                nc.vector.tensor_tensor(rot[:, :, a, 1, :], high[:], table(cos_sb, j, 1), ALU.mult)
-                nc.vector.tensor_tensor(crossed[:, :, a, 0, :], high[:], table(sin_sb, j, 0), ALU.mult)
-            rot_halves = rot[:].rearrange("p w a h c -> p (w a) h c")
-            crossed_halves = crossed[:].rearrange("p w a h c -> p (w a) h c")
-            for h, engine, op in ((0, nc.gpsimd, ALU.subtract), (1, nc.vector, ALU.add)):
-                engine.tensor_tensor(
-                    rot_halves[:, :, h, :], rot_halves[:, :, h, :], crossed_halves[:, :, h, :], op
-                )
+        units = [(s, b) for s in range(SWEEPS) for b in range(BATCH)]
+        turn_tables(0)
+        ready = quantise(*units[0])
+        for n, (s, b) in enumerate(units):
+            x_codes, x_scales = ready
             for w in range(WEIGHTS):
+                out_sb = rows.tile([P, TILES, 2, 2, P], F32, name="out_sb")
+                for r in range(2):
+                    pair = [products(s, w, r + 2 * h, x_codes, x_scales) for h in range(2)]
+                    if w == 0 and r == 0 and n + 1 < len(units):
+                        ready = quantise(*units[n + 1])
+                    if n == 1 and w == 1 and r == 0:
+                        turn_tables(1)
+                    for half in range(2):
+                        turned = back.tile([P, 2, 2, P], F32, name="turned_back")
+                        for a in range(2):
+                            tokens = slice((2 * half + a) * P, (2 * half + a + 1) * P)
+                            for h in range(2):
+                                nc.tensor.matmul(
+                                    out=turned[:, a, h, :], lhsT=pair[h][:, 0, tokens], rhs=ident[:],
+                                    is_transpose=True, start=True, stop=False,
+                                )
+                                nc.tensor.matmul(
+                                    out=turned[:, a, h, :], lhsT=pair[1 - h][:, 1, tokens], rhs=ident[:],
+                                    is_transpose=True, start=False, stop=True,
+                                )
+                        nc.scalar.copy(out=out_sb[:, 2 * half : 2 * half + 2, :, r, :], in_=turned[:])
                 out_rows = outs[w][b].rearrange("(p j) d -> p j d", j=ROWS)
                 nc.sync.dma_start(
-                    out=out_rows[:, j0 : j0 + PAIR, :],
-                    in_=rot[:, w].rearrange("p a h c -> p a (h c)"),
+                    out=out_rows[:, s * TILES : (s + 1) * TILES, :],
+                    in_=out_sb[:].rearrange("p a h r c -> p a (h r c)"),
                 )
-
-        ready = quantise(*groups[0])
-        for g, (b, j0) in enumerate(groups):
-            x_codes, x_scales = ready
-            if g + 1 < len(groups):
-                ready = quantise(*groups[g + 1])
-            rotate_and_store(b, j0, x_codes, x_scales)

@@ -19,9 +19,7 @@ WORDS = DIM // 2
 PACK = 4
 ROWS = SEQ // P
 CHUNKS = DIM // P
-TILES = 4
-UNIT = TILES * P
-SWEEPS = ROWS // TILES
+UNIT = BATCH * P
 WEIGHTS = 2
 
 FLOPS = 2 * BATCH * SEQ * DIM * WEIGHTS * DIM
@@ -40,20 +38,18 @@ def tile_attention_pa_t_kernel(
     tc, x, cos, sin, wq_words, wq_scales, wk_words, wk_scales, out_q, out_k
 ):
     nc = tc.nc
-    outs = (out_q, out_k)
+    out_rows = [o.rearrange("b (p j) d -> p b j d", j=ROWS) for o in (out_q, out_k)]
 
     with (
         tc.tile_pool(name="keep", bufs=1) as keep,
         tc.tile_pool(name="quant", bufs=2) as quant,
         tc.tile_pool(name="prods", bufs=6) as prods,
         tc.tile_pool(name="rows", bufs=3) as rows,
-        tc.psum_pool(name="flip", bufs=2) as flip,
+        tc.psum_pool(name="flip", bufs=1) as flip,
         tc.psum_pool(name="sums", bufs=4) as sums,
-        tc.psum_pool(name="back", bufs=2) as back,
+        tc.psum_pool(name="back", bufs=3) as back,
     ):
-        x_sb = keep.tile([P, BATCH, ROWS, DIM], BF16)
-        raw = keep.tile([P, 2, ROWS, DIM], BF16)
-        tables = keep.tile([P, CHUNKS, 2, SEQ], BF16)
+        tables = [keep.tile([P, CHUNKS, 2, P], BF16, name="tables%d" % j) for j in range(ROWS)]
         w_words = keep.tile([P, WEIGHTS, 2 * DIM], U8, align_bytes=64)
         w_scales = keep.tile([P, WEIGHTS, DIM], U8, align_bytes=64)
         ident = keep.tile([P, P], F32)
@@ -63,55 +59,56 @@ def tile_attention_pa_t_kernel(
         make_identity(nc, ident[:])
         make_identity(nc, ident_bf[:])
 
-        x_rows = [x[b].rearrange("(p j) d -> p j d", j=ROWS) for b in range(BATCH)]
+        x_rows = x.rearrange("b (p j) d -> p b j d", j=ROWS)
         table_rows = [t.rearrange("(p j) d -> p j d", j=ROWS) for t in (cos, sin)]
-        for s in range(SWEEPS):
-            piece = slice(s * TILES, (s + 1) * TILES)
-            for b in range(BATCH):
-                nc.sync.dma_start(out=x_sb[:, b, piece, :], in_=x_rows[b][:, piece, :])
-                if b == 0:
-                    if s == 0:
-                        load_weight(nc, wq_words, wq_scales, w_words, w_scales, 0)
-                        load_weight(nc, wk_words, wk_scales, w_words, w_scales, 1)
-                    for t in range(2):
-                        nc.sync.dma_start(out=raw[:, t, piece, :], in_=table_rows[t][:, piece, :])
+        x_of = {}
+        raw_of = {}
+        for j0, j1 in ((0, 1), (1, 2), (2, 4), (4, 6), (6, 8)):
+            x_piece = keep.tile([P, BATCH, j1 - j0, DIM], BF16, name="x%d" % j0)
+            nc.sync.dma_start(
+                out=x_piece[:].rearrange("p b j d -> p b (j d)"),
+                in_=x_rows[:, :, j0:j1, :].rearrange("p b j d -> p b (j d)"),
+            )
+            if j0 == 0:
+                load_weight(nc, wq_words, wq_scales, w_words, w_scales, 0)
+                load_weight(nc, wk_words, wk_scales, w_words, w_scales, 1)
+            raw_piece = [keep.tile([P, j1 - j0, DIM], BF16, name="raw%d_%d" % (t, j0)) for t in range(2)]
+            for t in range(2):
+                nc.sync.dma_start(out=raw_piece[t][:], in_=table_rows[t][:, j0:j1, :])
+            for j in range(j0, j1):
+                x_of[j] = x_piece[:, :, j - j0, :]
+                raw_of[j] = [raw_piece[t][:, j - j0, :] for t in range(2)]
 
-        def turn_tables(s):
-            for j in range(s * TILES, (s + 1) * TILES):
-                cols = slice(j * P, (j + 1) * P)
-                for t in range(2):
-                    turned = flip.tile([P, CHUNKS, P], BF16, name="flipped")
-                    for c in range(CHUNKS):
-                        nc.tensor.transpose(turned[:, c, :], raw[:, t, j, c * P : (c + 1) * P], ident_bf[:])
-                    if t == 0:
-                        engine_copy = nc.vector.tensor_copy if s == 0 else nc.scalar.copy
-                        engine_copy(out=tables[:, :, 0, cols], in_=turned[:])
-                    else:
-                        nc.scalar.copy(out=tables[:, 0:2, 1, cols], in_=turned[:, 2:4, :])
-                        nc.scalar.activation(
-                            out=tables[:, 2:4, 1, cols], in_=turned[:, 0:2, :], func=ACT.Copy, scale=-1.0
-                        )
+        def turn_tables(j, pool, name):
+            turned = pool.tile([P, 2, CHUNKS, P], BF16, name=name)
+            for t in range(2):
+                for c in range(CHUNKS):
+                    nc.tensor.transpose(turned[:, t, c, :], raw_of[j][t][:, c * P : (c + 1) * P], ident_bf[:])
+            nc.scalar.copy(out=tables[j][:, :, 0, :], in_=turned[:, 0])
+            nc.scalar.copy(out=tables[j][:, 0:2, 1, :], in_=turned[:, 1, 2:4, :])
+            nc.scalar.activation(out=tables[j][:, 2:4, 1, :], in_=turned[:, 1, 0:2, :], func=ACT.Copy, scale=-1.0)
 
-        def quantise(s, b):
-            grouped = quant.tile([P, UNIT * PACK], BF16, align_bytes=64)
-            for half in range(2):
-                flipped = flip.tile([P, 2, 2, P], F32, name="flipped")
-                for a in range(2):
-                    x_words = x_sb[:, b, s * TILES + 2 * half + a, :].bitcast(F32)
-                    for u in range(2):
-                        nc.tensor.transpose(flipped[:, a, u, :], x_words[:, u : WORDS : 2], ident[:])
-                nc.scalar.copy(
-                    out=grouped[:, half * 2 * P * PACK : (half + 1) * 2 * P * PACK]
-                    .bitcast(F32)
-                    .rearrange("p (a r u) -> p a r u", a=2, u=2),
-                    in_=flipped[:].rearrange("p a u r -> p a r u"),
-                )
-            x_codes = quant.tile([P, UNIT], U32, align_bytes=64)
-            x_scales = quant.tile([P, UNIT], U8, align_bytes=64)
+        def turn_x(j, half, grouped, pool, name):
+            flipped = pool.tile([P, 2, 2, P], F32, name=name)
+            for a in range(2):
+                x_words = x_of[j][:, 2 * half + a, :].bitcast(F32)
+                for u in range(2):
+                    nc.tensor.transpose(flipped[:, a, u, :], x_words[:, u : WORDS : 2], ident[:])
+            nc.scalar.copy(
+                out=grouped[:, half * 2 * P * PACK : (half + 1) * 2 * P * PACK]
+                .bitcast(F32)
+                .rearrange("p (a r u) -> p a r u", a=2, u=2),
+                in_=flipped[:].rearrange("p a u r -> p a r u"),
+            )
+
+        def quantise(grouped):
+            x_codes = quant.tile([P, UNIT], U32, align_bytes=64, name="x_codes")
+            x_scales = quant.tile([P, UNIT], U8, align_bytes=64, name="x_scales")
             nc.vector.quantize_mx(out=x_codes[:].bitcast(FP8X4), scales=x_scales[:], in_=grouped[:])
             return x_codes, x_scales
 
-        def products(s, w, c, x_codes, x_scales):
+        def project(w, c, operand):
+            x_codes, x_scales = operand
             bank = sums.tile([P, UNIT], F32, name="bank")
             nc.tensor.matmul_mx(
                 out=bank[:],
@@ -122,44 +119,65 @@ def tile_attention_pa_t_kernel(
                 start=True,
                 stop=True,
             )
-            prod = prods.tile([P, 2, UNIT], F32, name="prod")
+            return bank
+
+        def multiply(j, c, bank):
+            prod = prods.tile([P, 2, BATCH, P], F32, name="prod")
             nc.vector.tensor_tensor(
                 prod[:],
-                bank[:].unsqueeze(1).to_broadcast([P, 2, UNIT]),
-                tables[:, c, :, s * UNIT : (s + 1) * UNIT],
+                bank[:].rearrange("p (b r) -> p b r", b=BATCH).unsqueeze(1).to_broadcast([P, 2, BATCH, P]),
+                tables[j][:, c, :, :].unsqueeze(2).to_broadcast([P, 2, BATCH, P]),
                 ALU.mult,
             )
             return prod
 
-        units = [(s, b) for s in range(SWEEPS) for b in range(BATCH)]
-        turn_tables(0)
-        ready = quantise(*units[0])
-        for n, (s, b) in enumerate(units):
-            x_codes, x_scales = ready
-            for w in range(WEIGHTS):
-                out_sb = rows.tile([P, TILES, 2, 2, P], F32, name="out_sb")
-                for r in range(2):
-                    pair = [products(s, w, r + 2 * h, x_codes, x_scales) for h in range(2)]
-                    if w == 0 and r == 0 and n + 1 < len(units):
-                        ready = quantise(*units[n + 1])
-                    if n == 1 and w == 1 and r == 0:
-                        turn_tables(1)
-                    for half in range(2):
-                        turned = back.tile([P, 2, 2, P], F32, name="turned_back")
-                        for a in range(2):
-                            tokens = slice((2 * half + a) * P, (2 * half + a + 1) * P)
-                            for h in range(2):
-                                nc.tensor.matmul(
-                                    out=turned[:, a, h, :], lhsT=pair[h][:, 0, tokens], rhs=ident[:],
-                                    is_transpose=True, start=True, stop=False,
-                                )
-                                nc.tensor.matmul(
-                                    out=turned[:, a, h, :], lhsT=pair[1 - h][:, 1, tokens], rhs=ident[:],
-                                    is_transpose=True, start=False, stop=True,
-                                )
-                        nc.scalar.copy(out=out_sb[:, 2 * half : 2 * half + 2, :, r, :], in_=turned[:])
-                out_rows = outs[w][b].rearrange("(p j) d -> p j d", j=ROWS)
-                nc.sync.dma_start(
-                    out=out_rows[:, s * TILES : (s + 1) * TILES, :],
-                    in_=out_sb[:].rearrange("p a h r c -> p a (h r c)"),
-                )
+        def join(pair, out_sb, r):
+            for half in range(2):
+                turned = back.tile([P, 2, 2, P], F32, name="turned_back")
+                for a in range(2):
+                    for h in range(2):
+                        nc.tensor.matmul(
+                            out=turned[:, a, h, :], lhsT=pair[h][:, 0, 2 * half + a, :], rhs=ident[:],
+                            is_transpose=True, start=True, stop=False,
+                        )
+                        nc.tensor.matmul(
+                            out=turned[:, a, h, :], lhsT=pair[1 - h][:, 1, 2 * half + a, :], rhs=ident[:],
+                            is_transpose=True, start=False, stop=True,
+                        )
+                nc.scalar.copy(out=out_sb[:, 2 * half : 2 * half + 2, :, r, :], in_=turned[:])
+
+        steps = [(j, w, r) for j in range(ROWS) for w in range(WEIGHTS) for r in range(2)]
+
+        with tc.manual_schedule(engines={mybir.EngineType.PE}):
+            grouped = quant.tile([P, UNIT * PACK], BF16, align_bytes=64, name="grouped")
+            turn_x(0, 0, grouped, back, "turned_back")
+            turn_x(0, 1, grouped, back, "turned_back")
+            turn_tables(0, back, "turned_back")
+            operands = {0: quantise(grouped)}
+            banks = {0: [project(steps[0][1], steps[0][2] + 2 * h, operands[0]) for h in range(2)]}
+            pairs = {}
+            out_tiles = {}
+            for n, (j, w, r) in enumerate(steps):
+                if n + 1 < len(steps):
+                    j1, w1, r1 = steps[n + 1]
+                    banks[n + 1] = [project(w1, r1 + 2 * h, operands[j1]) for h in range(2)]
+                pairs[n] = [multiply(j, r + 2 * h, banks[n][h]) for h in range(2)]
+                if j + 1 < ROWS:
+                    if n % 4 == 0:
+                        grouped = quant.tile([P, UNIT * PACK], BF16, align_bytes=64, name="grouped")
+                        turn_x(j + 1, 0, grouped, flip, "flipped")
+                    elif n % 4 == 1:
+                        turn_x(j + 1, 1, grouped, flip, "flipped")
+                        operands[j + 1] = quantise(grouped)
+                    elif n % 4 == 2:
+                        turn_tables(j + 1, flip, "flipped")
+                for m in ([n - 1] if n > 0 else []) + ([n] if n + 1 == len(steps) else []):
+                    jm, wm, rm = steps[m]
+                    if rm == 0:
+                        out_tiles[wm] = rows.tile([P, BATCH, 2, 2, P], F32, name="out_sb")
+                    join(pairs[m], out_tiles[wm], rm)
+                    if rm == 1:
+                        nc.sync.dma_start(
+                            out=out_rows[wm][:, :, jm, :],
+                            in_=out_tiles[wm][:].rearrange("p b h r c -> p b (h r c)"),
+                        )

@@ -43,7 +43,7 @@ def tile_attention_pa_t_kernel(
     with (
         tc.tile_pool(name="keep", bufs=1) as keep,
         tc.tile_pool(name="quant", bufs=2) as quant,
-        tc.tile_pool(name="prods", bufs=6) as prods,
+        tc.tile_pool(name="prods", bufs=8) as prods,
         tc.tile_pool(name="rows", bufs=3) as rows,
         tc.psum_pool(name="flip", bufs=1) as flip,
         tc.psum_pool(name="sums", bufs=4) as sums,
@@ -146,38 +146,47 @@ def tile_attention_pa_t_kernel(
                         )
                 nc.scalar.copy(out=out_sb[:, 2 * half : 2 * half + 2, :, r, :], in_=turned[:])
 
-        steps = [(j, w, r) for j in range(ROWS) for w in range(WEIGHTS) for r in range(2)]
+        rounds = [(j, w) for j in range(ROWS) for w in range(WEIGHTS)]
+        order = [(r, h) for r in range(2) for h in range(2)]
+
+        def project_round(k, operands):
+            j, w = rounds[k]
+            return {(r, h): project(w, r + 2 * h, operands[j]) for r, h in order}
+
+        def multiply_round(k, banks):
+            j, w = rounds[k]
+            return {(r, h): multiply(j, r + 2 * h, banks[(r, h)]) for r, h in order}
 
         with tc.manual_schedule(engines={mybir.EngineType.PE}):
             grouped = quant.tile([P, UNIT * PACK], BF16, align_bytes=64, name="grouped")
             turn_x(0, 0, grouped, back, "turned_back")
             turn_x(0, 1, grouped, back, "turned_back")
-            turn_tables(0, back, "turned_back")
+            turn_tables(0, flip, "flipped")
             operands = {0: quantise(grouped)}
-            banks = {0: [project(steps[0][1], steps[0][2] + 2 * h, operands[0]) for h in range(2)]}
-            pairs = {}
-            out_tiles = {}
-            for n, (j, w, r) in enumerate(steps):
-                if n + 1 < len(steps):
-                    j1, w1, r1 = steps[n + 1]
-                    banks[n + 1] = [project(w1, r1 + 2 * h, operands[j1]) for h in range(2)]
-                pairs[n] = [multiply(j, r + 2 * h, banks[n][h]) for h in range(2)]
-                if j + 1 < ROWS:
-                    if n % 4 == 0:
-                        grouped = quant.tile([P, UNIT * PACK], BF16, align_bytes=64, name="grouped")
-                        turn_x(j + 1, 0, grouped, flip, "flipped")
-                    elif n % 4 == 1:
-                        turn_x(j + 1, 1, grouped, flip, "flipped")
-                        operands[j + 1] = quantise(grouped)
-                    elif n % 4 == 2:
-                        turn_tables(j + 1, flip, "flipped")
-                for m in ([n - 1] if n > 0 else []) + ([n] if n + 1 == len(steps) else []):
-                    jm, wm, rm = steps[m]
-                    if rm == 0:
-                        out_tiles[wm] = rows.tile([P, BATCH, 2, 2, P], F32, name="out_sb")
-                    join(pairs[m], out_tiles[wm], rm)
-                    if rm == 1:
-                        nc.sync.dma_start(
-                            out=out_rows[wm][:, :, jm, :],
-                            in_=out_tiles[wm][:].rearrange("p b h r c -> p b (h r c)"),
-                        )
+            banks = project_round(0, operands)
+            prod_of = {}
+            for k, (j, w) in enumerate(rounds):
+                prod_of[k] = multiply_round(k, banks)
+                more = j + 1 < ROWS
+                if more and w == 0:
+                    grouped = quant.tile([P, UNIT * PACK], BF16, align_bytes=64, name="grouped")
+                    turn_x(j + 1, 0, grouped, flip, "flipped")
+                if more and w == 1:
+                    turn_tables(j + 1, flip, "flipped")
+                for m in ([k - 1] if k > 0 else []) + ([k] if k + 1 == len(rounds) else []):
+                    jm, wm = rounds[m]
+                    out_sb = rows.tile([P, BATCH, 2, 2, P], F32, name="out_sb")
+                    for r in range(2):
+                        join([prod_of[m][(r, h)] for h in range(2)], out_sb, r)
+                        if r == 0 and m == k - 1 and more and w == 0:
+                            turn_x(j + 1, 1, grouped, flip, "flipped")
+                            operands[j + 1] = quantise(grouped)
+                    nc.sync.dma_start(
+                        out=out_rows[wm][:, :, jm, :],
+                        in_=out_sb[:].rearrange("p b h r c -> p b (h r c)"),
+                    )
+                if k == 0:
+                    turn_x(j + 1, 1, grouped, flip, "flipped")
+                    operands[j + 1] = quantise(grouped)
+                if k + 1 < len(rounds):
+                    banks = project_round(k + 1, operands)

@@ -19,8 +19,8 @@ WORDS = DIM // 2
 PACK = 4
 ROWS = SEQ // P
 CHUNKS = DIM // P
-UNIT = BATCH * P
 WEIGHTS = 2
+UNITS = ((0, 0, 2),) + tuple((j, 0, BATCH) for j in range(1, ROWS)) + ((0, 2, 2),)
 
 FLOPS = 2 * BATCH * SEQ * DIM * WEIGHTS * DIM
 
@@ -63,53 +63,71 @@ def tile_attention_pa_t_kernel(
         table_rows = [t.rearrange("(p j) d -> p j d", j=ROWS) for t in (cos, sin)]
         x_of = {}
         raw_of = {}
-        for j0, j1 in ((0, 1), (1, 2), (2, 4), (4, 6), (6, 8)):
-            x_piece = keep.tile([P, BATCH, j1 - j0, DIM], BF16, name="x%d" % j0)
+
+        def load_x(j0, j1, b0, nb):
+            piece = keep.tile([P, nb, j1 - j0, DIM], BF16, name="x%d_%d" % (j0, b0))
             nc.sync.dma_start(
-                out=x_piece[:].rearrange("p b j d -> p b (j d)"),
-                in_=x_rows[:, :, j0:j1, :].rearrange("p b j d -> p b (j d)"),
+                out=piece[:].rearrange("p b j d -> p b (j d)"),
+                in_=x_rows[:, b0 : b0 + nb, j0:j1, :].rearrange("p b j d -> p b (j d)"),
             )
-            if j0 == 0:
-                load_weight(nc, wq_words, wq_scales, w_words, w_scales, 0)
-                load_weight(nc, wk_words, wk_scales, w_words, w_scales, 1)
-            raw_piece = [keep.tile([P, j1 - j0, DIM], BF16, name="raw%d_%d" % (t, j0)) for t in range(2)]
-            for t in range(2):
-                nc.sync.dma_start(out=raw_piece[t][:], in_=table_rows[t][:, j0:j1, :])
             for j in range(j0, j1):
-                x_of[j] = x_piece[:, :, j - j0, :]
-                raw_of[j] = [raw_piece[t][:, j - j0, :] for t in range(2)]
+                for b in range(nb):
+                    x_of[(j, b0 + b)] = piece[:, b, j - j0, :]
+
+        def load_tables(j0, j1):
+            for t in range(2):
+                piece = keep.tile([P, j1 - j0, DIM], BF16, name="raw%d_%d" % (t, j0))
+                nc.sync.dma_start(out=piece[:], in_=table_rows[t][:, j0:j1, :])
+                for j in range(j0, j1):
+                    raw_of[(j, t)] = piece[:, j - j0, :]
+
+        load_x(0, 1, 0, 2)
+        load_weight(nc, wq_words, wq_scales, w_words, w_scales, 0)
+        load_tables(0, 1)
+        load_x(1, 2, 0, BATCH)
+        load_weight(nc, wk_words, wk_scales, w_words, w_scales, 1)
+        load_tables(1, 2)
+        for j0 in (2, 4, 6):
+            load_x(j0, j0 + 2, 0, BATCH)
+            load_tables(j0, j0 + 2)
+        load_x(0, 1, 2, 2)
 
         def turn_tables(j, pool, name):
             turned = pool.tile([P, 2, CHUNKS, P], BF16, name=name)
             for t in range(2):
                 for c in range(CHUNKS):
-                    nc.tensor.transpose(turned[:, t, c, :], raw_of[j][t][:, c * P : (c + 1) * P], ident_bf[:])
+                    nc.tensor.transpose(turned[:, t, c, :], raw_of[(j, t)][:, c * P : (c + 1) * P], ident_bf[:])
             nc.scalar.copy(out=tables[j][:, :, 0, :], in_=turned[:, 0])
             nc.scalar.copy(out=tables[j][:, 0:2, 1, :], in_=turned[:, 1, 2:4, :])
             nc.scalar.activation(out=tables[j][:, 2:4, 1, :], in_=turned[:, 1, 0:2, :], func=ACT.Copy, scale=-1.0)
 
-        def turn_x(j, half, grouped, pool, name):
+        def turn_x(u, slot, grouped, pool, name):
+            j, b0, nb = UNITS[u]
             flipped = pool.tile([P, 2, 2, P], F32, name=name)
             for a in range(2):
-                x_words = x_of[j][:, 2 * half + a, :].bitcast(F32)
-                for u in range(2):
-                    nc.tensor.transpose(flipped[:, a, u, :], x_words[:, u : WORDS : 2], ident[:])
+                x_words = x_of[(j, b0 + 2 * slot + a)].bitcast(F32)
+                for e in range(2):
+                    nc.tensor.transpose(flipped[:, a, e, :], x_words[:, e : WORDS : 2], ident[:])
             nc.scalar.copy(
-                out=grouped[:, half * 2 * P * PACK : (half + 1) * 2 * P * PACK]
+                out=grouped[:, slot * 2 * P * PACK : (slot + 1) * 2 * P * PACK]
                 .bitcast(F32)
-                .rearrange("p (a r u) -> p a r u", a=2, u=2),
-                in_=flipped[:].rearrange("p a u r -> p a r u"),
+                .rearrange("p (a r e) -> p a r e", a=2, e=2),
+                in_=flipped[:].rearrange("p a e r -> p a r e"),
             )
 
-        def quantise(grouped):
-            x_codes = quant.tile([P, UNIT], U32, align_bytes=64, name="x_codes")
-            x_scales = quant.tile([P, UNIT], U8, align_bytes=64, name="x_scales")
+        def new_grouped(u):
+            return quant.tile([P, UNITS[u][2] * P * PACK], BF16, align_bytes=64, name="grouped")
+
+        def quantise(u, grouped):
+            tokens = UNITS[u][2] * P
+            x_codes = quant.tile([P, tokens], U32, align_bytes=64, name="x_codes")
+            x_scales = quant.tile([P, tokens], U8, align_bytes=64, name="x_scales")
             nc.vector.quantize_mx(out=x_codes[:].bitcast(FP8X4), scales=x_scales[:], in_=grouped[:])
             return x_codes, x_scales
 
-        def project(w, c, operand):
+        def project(u, w, c, operand):
             x_codes, x_scales = operand
-            bank = sums.tile([P, UNIT], F32, name="bank")
+            bank = sums.tile([P, UNITS[u][2] * P], F32, name="bank")
             nc.tensor.matmul_mx(
                 out=bank[:],
                 lhsT=w_words[:, w, c * 2 * P : (c + 1) * 2 * P].bitcast(FP4X4),
@@ -121,18 +139,19 @@ def tile_attention_pa_t_kernel(
             )
             return bank
 
-        def multiply(j, c, bank):
-            prod = prods.tile([P, 2, BATCH, P], F32, name="prod")
+        def multiply(u, c, bank):
+            j, b0, nb = UNITS[u]
+            prod = prods.tile([P, 2, nb, P], F32, name="prod")
             nc.vector.tensor_tensor(
                 prod[:],
-                bank[:].rearrange("p (b r) -> p b r", b=BATCH).unsqueeze(1).to_broadcast([P, 2, BATCH, P]),
-                tables[j][:, c, :, :].unsqueeze(2).to_broadcast([P, 2, BATCH, P]),
+                bank[:].rearrange("p (b r) -> p b r", b=nb).unsqueeze(1).to_broadcast([P, 2, nb, P]),
+                tables[j][:, c, :, :].unsqueeze(2).to_broadcast([P, 2, nb, P]),
                 ALU.mult,
             )
             return prod
 
-        def join(pair, out_sb, r):
-            for half in range(2):
+        def join(u, pair, out_sb, r):
+            for half in range(UNITS[u][2] // 2):
                 turned = back.tile([P, 2, 2, P], F32, name="turned_back")
                 for a in range(2):
                     for h in range(2):
@@ -146,47 +165,58 @@ def tile_attention_pa_t_kernel(
                         )
                 nc.scalar.copy(out=out_sb[:, 2 * half : 2 * half + 2, :, r, :], in_=turned[:])
 
-        rounds = [(j, w) for j in range(ROWS) for w in range(WEIGHTS)]
+        rounds = [(u, w) for u in range(len(UNITS)) for w in range(WEIGHTS)]
         order = [(r, h) for r in range(2) for h in range(2)]
+        operands = {}
 
-        def project_round(k, operands):
-            j, w = rounds[k]
-            return {(r, h): project(w, r + 2 * h, operands[j]) for r, h in order}
+        def project_round(k, wanted=(0, 1)):
+            u, w = rounds[k]
+            return {(r, h): project(u, w, r + 2 * h, operands[u]) for r, h in order if r in wanted}
 
         def multiply_round(k, banks):
-            j, w = rounds[k]
-            return {(r, h): multiply(j, r + 2 * h, banks[(r, h)]) for r, h in order}
+            u, w = rounds[k]
+            return {(r, h): multiply(u, r + 2 * h, banks[(r, h)]) for r, h in order}
 
         with tc.manual_schedule(engines={mybir.EngineType.PE}):
-            grouped = quant.tile([P, UNIT * PACK], BF16, align_bytes=64, name="grouped")
+            grouped = new_grouped(0)
             turn_x(0, 0, grouped, back, "turned_back")
-            turn_x(0, 1, grouped, back, "turned_back")
-            turn_tables(0, flip, "flipped")
-            operands = {0: quantise(grouped)}
-            banks = project_round(0, operands)
+            operands[0] = quantise(0, grouped)
+            turn_tables(UNITS[0][0], flip, "flipped")
+            banks = project_round(0)
             prod_of = {}
-            for k, (j, w) in enumerate(rounds):
+            for k, (u, w) in enumerate(rounds):
                 prod_of[k] = multiply_round(k, banks)
-                more = j + 1 < ROWS
+                if k == 0:
+                    grouped = new_grouped(1)
+                    turn_x(1, 0, grouped, back, "turned_back")
+                    banks = project_round(1, (0,))
+                    turn_x(1, 1, grouped, back, "turned_back")
+                    operands[1] = quantise(1, grouped)
+                    late = project_round(1, (1,))
+                    for key in late:
+                        banks[key] = late[key]
+                    continue
+                more = u + 1 < len(UNITS)
+                second = more and w == 0 and UNITS[u + 1][2] == BATCH
                 if more and w == 0:
-                    grouped = quant.tile([P, UNIT * PACK], BF16, align_bytes=64, name="grouped")
-                    turn_x(j + 1, 0, grouped, flip, "flipped")
-                if more and w == 1:
-                    turn_tables(j + 1, flip, "flipped")
+                    grouped = new_grouped(u + 1)
+                    turn_x(u + 1, 0, grouped, flip, "flipped")
+                    if not second:
+                        operands[u + 1] = quantise(u + 1, grouped)
+                if more and w == 1 and UNITS[u + 1][0] != UNITS[0][0]:
+                    turn_tables(UNITS[u + 1][0], flip, "flipped")
                 for m in ([k - 1] if k > 0 else []) + ([k] if k + 1 == len(rounds) else []):
-                    jm, wm = rounds[m]
-                    out_sb = rows.tile([P, BATCH, 2, 2, P], F32, name="out_sb")
+                    um, wm = rounds[m]
+                    jm, b0, nb = UNITS[um]
+                    out_sb = rows.tile([P, nb, 2, 2, P], F32, name="out_sb")
                     for r in range(2):
-                        join([prod_of[m][(r, h)] for h in range(2)], out_sb, r)
-                        if r == 0 and m == k - 1 and more and w == 0:
-                            turn_x(j + 1, 1, grouped, flip, "flipped")
-                            operands[j + 1] = quantise(grouped)
+                        join(um, [prod_of[m][(r, h)] for h in range(2)], out_sb, r)
+                        if r == 0 and m == k - 1 and second:
+                            turn_x(u + 1, 1, grouped, flip, "flipped")
+                            operands[u + 1] = quantise(u + 1, grouped)
                     nc.sync.dma_start(
-                        out=out_rows[wm][:, :, jm, :],
+                        out=out_rows[wm][:, b0 : b0 + nb, jm, :],
                         in_=out_sb[:].rearrange("p b h r c -> p b (h r c)"),
                     )
-                if k == 0:
-                    turn_x(j + 1, 1, grouped, flip, "flipped")
-                    operands[j + 1] = quantise(grouped)
                 if k + 1 < len(rounds):
-                    banks = project_round(k + 1, operands)
+                    banks = project_round(k + 1)

@@ -15,22 +15,30 @@ P = 128
 BATCH = 4
 SEQ = 1024
 DIM = 512
+HALF = DIM // 2
 WORDS = DIM // 2
 PACK = 4
 ROWS = SEQ // P
 CHUNKS = DIM // P
 WEIGHTS = 2
-UNITS = ((0, 0, 2),) + tuple((j, 0, BATCH) for j in range(1, ROWS)) + ((0, 2, 2),)
+UNITS = ((0, 0, 2),) + tuple((j, 0, BATCH) for j in range(2, ROWS)) + ((0, 2, 2),)
+PLAIN = (1, 0, BATCH)
+FIRST_GATE = 3
 
 FLOPS = 2 * BATCH * SEQ * DIM * WEIGHTS * DIM
 
 
 def load_weight(nc, words_dram, scales_dram, words, scales, w):
-    nc.sync.dma_start(out=words[:, w, :].bitcast(I32), in_=words_dram[0].bitcast(I32))
+    nc.sync.dma_start(
+        out=words[:, :, w, :].bitcast(I32),
+        in_=words_dram[0].bitcast(I32).rearrange("p (h c) -> p h c", h=2),
+    )
     for quadrant in range(4):
         nc.sync.dma_start(
-            out=scales[32 * quadrant : 32 * quadrant + 4, w, :].bitcast(I32),
-            in_=scales_dram[0, 4 * quadrant : 4 * quadrant + 4, :].bitcast(I32),
+            out=scales[32 * quadrant : 32 * quadrant + 4, :, w, :].bitcast(I32),
+            in_=scales_dram[0, 4 * quadrant : 4 * quadrant + 4, :]
+            .bitcast(I32)
+            .rearrange("q (h c) -> q h c", h=2),
         )
 
 
@@ -45,13 +53,14 @@ def tile_attention_pa_t_kernel(
         tc.tile_pool(name="quant", bufs=2) as quant,
         tc.tile_pool(name="prods", bufs=8) as prods,
         tc.tile_pool(name="rows", bufs=3) as rows,
+        tc.tile_pool(name="plain", bufs=2) as plain,
         tc.psum_pool(name="flip", bufs=1) as flip,
         tc.psum_pool(name="sums", bufs=4) as sums,
         tc.psum_pool(name="back", bufs=3) as back,
     ):
-        tables = [keep.tile([P, CHUNKS, 2, P], BF16, name="tables%d" % j) for j in range(ROWS)]
-        w_words = keep.tile([P, WEIGHTS, 2 * DIM], U8, align_bytes=64)
-        w_scales = keep.tile([P, WEIGHTS, DIM], U8, align_bytes=64)
+        tables = {j: keep.tile([P, CHUNKS, 2, P], BF16, name="tables%d" % j) for j in range(ROWS) if j != PLAIN[0]}
+        w_words = keep.tile([P, 2, WEIGHTS, 2 * HALF], U8, align_bytes=64)
+        w_scales = keep.tile([P, 2, WEIGHTS, HALF], U8, align_bytes=64)
         ident = keep.tile([P, P], F32)
         ident_bf = keep.tile([P, P], BF16)
 
@@ -84,10 +93,14 @@ def tile_attention_pa_t_kernel(
         load_x(0, 1, 0, 2)
         load_weight(nc, wq_words, wq_scales, w_words, w_scales, 0)
         load_tables(0, 1)
-        load_x(1, 2, 0, BATCH)
+        load_x(2, 3, 0, BATCH)
         load_weight(nc, wk_words, wk_scales, w_words, w_scales, 1)
+        load_tables(2, 3)
+        load_x(1, 2, 0, BATCH)
         load_tables(1, 2)
-        for j0 in (2, 4, 6):
+        load_x(3, 4, 0, BATCH)
+        load_tables(3, 4)
+        for j0 in (4, 6):
             load_x(j0, j0 + 2, 0, BATCH)
             load_tables(j0, j0 + 2)
         load_x(0, 1, 2, 2)
@@ -101,8 +114,8 @@ def tile_attention_pa_t_kernel(
             nc.scalar.copy(out=tables[j][:, 0:2, 1, :], in_=turned[:, 1, 2:4, :])
             nc.scalar.activation(out=tables[j][:, 2:4, 1, :], in_=turned[:, 1, 0:2, :], func=ACT.Copy, scale=-1.0)
 
-        def turn_x(u, slot, grouped, pool, name):
-            j, b0, nb = UNITS[u]
+        def turn_x(unit, slot, grouped, pool, name):
+            j, b0, nb = unit
             flipped = pool.tile([P, 2, 2, P], F32, name=name)
             for a in range(2):
                 x_words = x_of[(j, b0 + 2 * slot + a)].bitcast(F32)
@@ -115,23 +128,23 @@ def tile_attention_pa_t_kernel(
                 in_=flipped[:].rearrange("p a e r -> p a r e"),
             )
 
-        def new_grouped(u):
-            return quant.tile([P, UNITS[u][2] * P * PACK], BF16, align_bytes=64, name="grouped")
+        def new_grouped(unit, pool):
+            return pool.tile([P, unit[2] * P * PACK], BF16, align_bytes=64, name="grouped")
 
-        def quantise(u, grouped):
-            tokens = UNITS[u][2] * P
-            x_codes = quant.tile([P, tokens], U32, align_bytes=64, name="x_codes")
-            x_scales = quant.tile([P, tokens], U8, align_bytes=64, name="x_scales")
+        def quantise(unit, grouped, pool):
+            tokens = unit[2] * P
+            x_codes = pool.tile([P, tokens], U32, align_bytes=64, name="x_codes")
+            x_scales = pool.tile([P, tokens], U8, align_bytes=64, name="x_scales")
             nc.vector.quantize_mx(out=x_codes[:].bitcast(FP8X4), scales=x_scales[:], in_=grouped[:])
             return x_codes, x_scales
 
-        def project(u, w, c, operand):
+        def project(unit, w, r, h, operand):
             x_codes, x_scales = operand
-            bank = sums.tile([P, UNITS[u][2] * P], F32, name="bank")
+            bank = sums.tile([P, unit[2] * P], F32, name="bank")
             nc.tensor.matmul_mx(
                 out=bank[:],
-                lhsT=w_words[:, w, c * 2 * P : (c + 1) * 2 * P].bitcast(FP4X4),
-                lhsT_scale=w_scales[:, w, c * P : (c + 1) * P],
+                lhsT=w_words[:, h, w, r * 2 * P : (r + 1) * 2 * P].bitcast(FP4X4),
+                lhsT_scale=w_scales[:, h, w, r * P : (r + 1) * P],
                 rhs=x_codes[:].bitcast(FP8X4),
                 rhs_scale=x_scales[:],
                 start=True,
@@ -139,8 +152,8 @@ def tile_attention_pa_t_kernel(
             )
             return bank
 
-        def multiply(u, c, bank):
-            j, b0, nb = UNITS[u]
+        def multiply(unit, c, bank):
+            j, b0, nb = unit
             prod = prods.tile([P, 2, nb, P], F32, name="prod")
             nc.vector.tensor_tensor(
                 prod[:],
@@ -150,8 +163,8 @@ def tile_attention_pa_t_kernel(
             )
             return prod
 
-        def join(u, pair, out_sb, r):
-            for half in range(UNITS[u][2] // 2):
+        def join(unit, pair, out_sb, r):
+            for half in range(unit[2] // 2):
                 turned = back.tile([P, 2, 2, P], F32, name="turned_back")
                 for a in range(2):
                     for h in range(2):
@@ -165,33 +178,77 @@ def tile_attention_pa_t_kernel(
                         )
                 nc.scalar.copy(out=out_sb[:, 2 * half : 2 * half + 2, :, r, :], in_=turned[:])
 
+        def plain_project(b, operand):
+            x_codes, x_scales = operand
+            sums_sb = plain.tile([P, 2, WEIGHTS * HALF], F32, name="sums_sb")
+            for h in range(2):
+                bank = sums.tile([P, WEIGHTS * HALF], F32, name="bank")
+                nc.tensor.matmul_mx(
+                    out=bank[:],
+                    lhsT=x_codes[:, b * P : (b + 1) * P].bitcast(FP8X4),
+                    lhsT_scale=x_scales[:, b * P : (b + 1) * P],
+                    rhs=w_words[:, h].rearrange("p w c -> p (w c)").bitcast(FP4X4),
+                    rhs_scale=w_scales[:, h].rearrange("p w c -> p (w c)"),
+                    start=True,
+                    stop=True,
+                )
+                nc.scalar.copy(out=sums_sb[:, h, :], in_=bank[:])
+            return sums_sb
+
+        def plain_rotate(b, sums_sb, operand):
+            j = PLAIN[0]
+
+            def table(t, h):
+                return raw_of[(j, t)][:, h * HALF : (h + 1) * HALF].unsqueeze(1).to_broadcast([P, WEIGHTS, HALF])
+
+            waited = plain.tile([P, 16], U32, name="waited")
+            nc.gpsimd.tensor_copy(out=waited[:], in_=operand[0][:, 0:16])
+            low = sums_sb[:, 0, :].rearrange("p (w c) -> p w c", w=WEIGHTS)
+            high = sums_sb[:, 1, :].rearrange("p (w c) -> p w c", w=WEIGHTS)
+            rot = plain.tile([P, WEIGHTS, 2, HALF], F32, name="rot")
+            crossed = plain.tile([P, WEIGHTS, 2, HALF], F32, name="crossed")
+            nc.gpsimd.tensor_tensor(rot[:, :, 0, :], low, table(0, 0), ALU.mult)
+            nc.gpsimd.tensor_tensor(crossed[:, :, 1, :], low, table(1, 1), ALU.mult)
+            nc.gpsimd.tensor_tensor(rot[:, :, 1, :], high, table(0, 1), ALU.mult)
+            nc.gpsimd.tensor_tensor(crossed[:, :, 0, :], high, table(1, 0), ALU.mult)
+            nc.gpsimd.tensor_tensor(rot[:, :, 0, :], rot[:, :, 0, :], crossed[:, :, 0, :], ALU.subtract)
+            nc.gpsimd.tensor_tensor(rot[:, :, 1, :], rot[:, :, 1, :], crossed[:, :, 1, :], ALU.add)
+            for w in range(WEIGHTS):
+                nc.gpsimd.dma_start(out=out_rows[w][:, b, j, :], in_=rot[:, w].rearrange("p h c -> p (h c)"))
+
         rounds = [(u, w) for u in range(len(UNITS)) for w in range(WEIGHTS)]
         order = [(r, h) for r in range(2) for h in range(2)]
         operands = {}
+        handed = {}
 
         def project_round(k, wanted=(0, 1)):
             u, w = rounds[k]
-            return {(r, h): project(u, w, r + 2 * h, operands[u]) for r, h in order if r in wanted}
+            return {(r, h): project(UNITS[u], w, r, h, operands[u]) for r, h in order if r in wanted}
 
         def multiply_round(k, banks):
             u, w = rounds[k]
-            return {(r, h): multiply(u, r + 2 * h, banks[(r, h)]) for r, h in order}
+            return {(r, h): multiply(UNITS[u], r + 2 * h, banks[(r, h)]) for r, h in order}
 
-        with tc.manual_schedule(engines={mybir.EngineType.PE}):
-            grouped = new_grouped(0)
-            turn_x(0, 0, grouped, back, "turned_back")
-            operands[0] = quantise(0, grouped)
+        def quantised(u, grouped):
+            operands[u] = quantise(UNITS[u], grouped, quant)
+            if u - FIRST_GATE in handed:
+                plain_rotate(u - FIRST_GATE, handed[u - FIRST_GATE], operands[u])
+
+        with tc.manual_schedule(engines={mybir.EngineType.PE, mybir.EngineType.Pool}):
+            grouped = new_grouped(UNITS[0], quant)
+            turn_x(UNITS[0], 0, grouped, back, "turned_back")
+            quantised(0, grouped)
             turn_tables(UNITS[0][0], flip, "flipped")
             banks = project_round(0)
             prod_of = {}
             for k, (u, w) in enumerate(rounds):
                 prod_of[k] = multiply_round(k, banks)
                 if k == 0:
-                    grouped = new_grouped(1)
-                    turn_x(1, 0, grouped, back, "turned_back")
+                    grouped = new_grouped(UNITS[1], quant)
+                    turn_x(UNITS[1], 0, grouped, back, "turned_back")
                     banks = project_round(1, (0,))
-                    turn_x(1, 1, grouped, back, "turned_back")
-                    operands[1] = quantise(1, grouped)
+                    turn_x(UNITS[1], 1, grouped, back, "turned_back")
+                    quantised(1, grouped)
                     late = project_round(1, (1,))
                     for key in late:
                         banks[key] = late[key]
@@ -199,24 +256,32 @@ def tile_attention_pa_t_kernel(
                 more = u + 1 < len(UNITS)
                 second = more and w == 0 and UNITS[u + 1][2] == BATCH
                 if more and w == 0:
-                    grouped = new_grouped(u + 1)
-                    turn_x(u + 1, 0, grouped, flip, "flipped")
+                    grouped = new_grouped(UNITS[u + 1], quant)
+                    turn_x(UNITS[u + 1], 0, grouped, flip, "flipped")
                     if not second:
-                        operands[u + 1] = quantise(u + 1, grouped)
+                        quantised(u + 1, grouped)
                 if more and w == 1 and UNITS[u + 1][0] != UNITS[0][0]:
                     turn_tables(UNITS[u + 1][0], flip, "flipped")
+                if k == 1:
+                    grouped_p = new_grouped(PLAIN, plain)
                 for m in ([k - 1] if k > 0 else []) + ([k] if k + 1 == len(rounds) else []):
                     um, wm = rounds[m]
                     jm, b0, nb = UNITS[um]
                     out_sb = rows.tile([P, nb, 2, 2, P], F32, name="out_sb")
                     for r in range(2):
-                        join(um, [prod_of[m][(r, h)] for h in range(2)], out_sb, r)
+                        join(UNITS[um], [prod_of[m][(r, h)] for h in range(2)], out_sb, r)
                         if r == 0 and m == k - 1 and second:
-                            turn_x(u + 1, 1, grouped, flip, "flipped")
-                            operands[u + 1] = quantise(u + 1, grouped)
+                            turn_x(UNITS[u + 1], 1, grouped, flip, "flipped")
+                            quantised(u + 1, grouped)
+                        if k == 1:
+                            turn_x(PLAIN, r, grouped_p, back, "turned_back")
                     nc.sync.dma_start(
                         out=out_rows[wm][:, b0 : b0 + nb, jm, :],
                         in_=out_sb[:].rearrange("p b h r c -> p b (h r c)"),
                     )
+                if k == 1:
+                    operand_p = quantise(PLAIN, grouped_p, plain)
+                if w == 1 and 0 <= (k - 3) // 2 < PLAIN[2]:
+                    handed[(k - 3) // 2] = plain_project((k - 3) // 2, operand_p)
                 if k + 1 < len(rounds):
                     banks = project_round(k + 1)

@@ -21,9 +21,13 @@ PACK = 4
 ROWS = SEQ // P
 CHUNKS = DIM // P
 WEIGHTS = 2
-UNITS = ((0, 0, 2),) + tuple((j, 0, BATCH) for j in range(2, ROWS)) + ((0, 2, 2),)
-PLAIN = (1, 0, BATCH)
-FIRST_GATE = 3
+OPERANDS = (((0, 0),),) + tuple(((j, 0), (j, 2)) for j in range(2, 7)) + (((7, 2), (0, 2)),)
+UNITS = ((0, 0, 2, 0, 0),) + tuple((j, 0, BATCH, j - 1, 0) for j in range(2, 7)) + ((7, 2, 2, 6, 0), (0, 2, 2, 6, 1))
+PLAIN_OPERANDS = (((1, 0), (1, 2)), ((7, 0),))
+PLAIN_TILES = tuple((1, b, 0, b) for b in range(BATCH)) + ((7, 0, 1, 0), (7, 1, 1, 1))
+GATED = {2: (0,), 3: (1,), 4: (2,), 5: (3,), 6: (4,)}
+PROJECTED = {2: 0, 3: 1, 5: 2, 7: 3, 9: 4, 11: 5}
+STORED = {4: 0, 6: 1, 8: 2, 10: 3, 13: 4, 15: 5}
 
 FLOPS = 2 * BATCH * SEQ * DIM * WEIGHTS * DIM
 
@@ -54,11 +58,12 @@ def tile_attention_pa_t_kernel(
         tc.tile_pool(name="prods", bufs=8) as prods,
         tc.tile_pool(name="rows", bufs=3) as rows,
         tc.tile_pool(name="plain", bufs=2) as plain,
+        tc.tile_pool(name="handover", bufs=3) as handover,
         tc.psum_pool(name="flip", bufs=1) as flip,
         tc.psum_pool(name="sums", bufs=4) as sums,
         tc.psum_pool(name="back", bufs=3) as back,
     ):
-        tables = {j: keep.tile([P, CHUNKS, 2, P], BF16, name="tables%d" % j) for j in range(ROWS) if j != PLAIN[0]}
+        tables = {j: keep.tile([P, CHUNKS, 2, P], BF16, name="tables%d" % j) for j in range(ROWS) if j != 1}
         w_words = keep.tile([P, 2, WEIGHTS, 2 * HALF], U8, align_bytes=64)
         w_scales = keep.tile([P, 2, WEIGHTS, HALF], U8, align_bytes=64)
         ident = keep.tile([P, P], F32)
@@ -114,11 +119,11 @@ def tile_attention_pa_t_kernel(
             nc.scalar.copy(out=tables[j][:, 0:2, 1, :], in_=turned[:, 1, 2:4, :])
             nc.scalar.activation(out=tables[j][:, 2:4, 1, :], in_=turned[:, 1, 0:2, :], func=ACT.Copy, scale=-1.0)
 
-        def turn_x(unit, slot, grouped, pool, name):
-            j, b0, nb = unit
+        def turn_x(pair, slot, grouped, pool, name):
+            j, b = pair
             flipped = pool.tile([P, 2, 2, P], F32, name=name)
             for a in range(2):
-                x_words = x_of[(j, b0 + 2 * slot + a)].bitcast(F32)
+                x_words = x_of[(j, b + a)].bitcast(F32)
                 for e in range(2):
                     nc.tensor.transpose(flipped[:, a, e, :], x_words[:, e : WORDS : 2], ident[:])
             nc.scalar.copy(
@@ -128,32 +133,39 @@ def tile_attention_pa_t_kernel(
                 in_=flipped[:].rearrange("p a e r -> p a r e"),
             )
 
-        def new_grouped(unit, pool):
-            return pool.tile([P, unit[2] * P * PACK], BF16, align_bytes=64, name="grouped")
+        def new_grouped(pairs, pool):
+            return pool.tile([P, len(pairs) * 2 * P * PACK], BF16, align_bytes=64, name="grouped")
 
-        def quantise(unit, grouped, pool):
-            tokens = unit[2] * P
+        def quantise(pairs, grouped, pool):
+            tokens = len(pairs) * 2 * P
             x_codes = pool.tile([P, tokens], U32, align_bytes=64, name="x_codes")
             x_scales = pool.tile([P, tokens], U8, align_bytes=64, name="x_scales")
             nc.vector.quantize_mx(out=x_codes[:].bitcast(FP8X4), scales=x_scales[:], in_=grouped[:])
             return x_codes, x_scales
 
-        def project(unit, w, r, h, operand):
-            x_codes, x_scales = operand
-            bank = sums.tile([P, unit[2] * P], F32, name="bank")
+        operands = {}
+        plain_operands = {}
+        handed = {}
+        rotated = {}
+
+        def project(unit, w, r, h):
+            j, b0, nb, operand, first = unit
+            x_codes, x_scales = operands[operand]
+            tokens = slice(first * 2 * P, first * 2 * P + nb * P)
+            bank = sums.tile([P, nb * P], F32, name="bank")
             nc.tensor.matmul_mx(
                 out=bank[:],
                 lhsT=w_words[:, h, w, r * 2 * P : (r + 1) * 2 * P].bitcast(FP4X4),
                 lhsT_scale=w_scales[:, h, w, r * P : (r + 1) * P],
-                rhs=x_codes[:].bitcast(FP8X4),
-                rhs_scale=x_scales[:],
+                rhs=x_codes[:, tokens].bitcast(FP8X4),
+                rhs_scale=x_scales[:, tokens],
                 start=True,
                 stop=True,
             )
             return bank
 
         def multiply(unit, c, bank):
-            j, b0, nb = unit
+            j, nb = unit[0], unit[2]
             prod = prods.tile([P, 2, nb, P], F32, name="prod")
             nc.vector.tensor_tensor(
                 prod[:],
@@ -163,8 +175,10 @@ def tile_attention_pa_t_kernel(
             )
             return prod
 
-        def join(unit, pair, out_sb, r):
+        def join(unit, pair, out_sb, r, before_last=None):
             for half in range(unit[2] // 2):
+                if before_last is not None and half == unit[2] // 2 - 1:
+                    plain_project(before_last)
                 turned = back.tile([P, 2, 2, P], F32, name="turned_back")
                 for a in range(2):
                     for h in range(2):
@@ -178,31 +192,34 @@ def tile_attention_pa_t_kernel(
                         )
                 nc.scalar.copy(out=out_sb[:, 2 * half : 2 * half + 2, :, r, :], in_=turned[:])
 
-        def plain_project(b, operand):
-            x_codes, x_scales = operand
-            sums_sb = plain.tile([P, 2, WEIGHTS * HALF], F32, name="sums_sb")
+        def plain_project(i):
+            j, b, operand, a = PLAIN_TILES[i]
+            x_codes, x_scales = plain_operands[operand]
+            sums_sb = handover.tile([P, 2, WEIGHTS * HALF], F32, name="sums_sb")
             for h in range(2):
                 bank = sums.tile([P, WEIGHTS * HALF], F32, name="bank")
                 nc.tensor.matmul_mx(
                     out=bank[:],
-                    lhsT=x_codes[:, b * P : (b + 1) * P].bitcast(FP8X4),
-                    lhsT_scale=x_scales[:, b * P : (b + 1) * P],
+                    lhsT=x_codes[:, a * P : (a + 1) * P].bitcast(FP8X4),
+                    lhsT_scale=x_scales[:, a * P : (a + 1) * P],
                     rhs=w_words[:, h].rearrange("p w c -> p (w c)").bitcast(FP4X4),
                     rhs_scale=w_scales[:, h].rearrange("p w c -> p (w c)"),
                     start=True,
                     stop=True,
                 )
                 nc.scalar.copy(out=sums_sb[:, h, :], in_=bank[:])
-            return sums_sb
+            handed[i] = sums_sb
 
-        def plain_rotate(b, sums_sb, operand):
-            j = PLAIN[0]
+        def plain_rotate(i, behind):
+            j, b = PLAIN_TILES[i][0], PLAIN_TILES[i][1]
+            sums_sb = handed[i]
 
             def table(t, h):
                 return raw_of[(j, t)][:, h * HALF : (h + 1) * HALF].unsqueeze(1).to_broadcast([P, WEIGHTS, HALF])
 
-            waited = plain.tile([P, 16], U32, name="waited")
-            nc.gpsimd.tensor_copy(out=waited[:], in_=operand[0][:, 0:16])
+            if behind is not None:
+                waited = plain.tile([P, 16], U32, name="waited")
+                nc.gpsimd.tensor_copy(out=waited[:], in_=behind[0][:, 0:16])
             low = sums_sb[:, 0, :].rearrange("p (w c) -> p w c", w=WEIGHTS)
             high = sums_sb[:, 1, :].rearrange("p (w c) -> p w c", w=WEIGHTS)
             rot = plain.tile([P, WEIGHTS, 2, HALF], F32, name="rot")
@@ -213,75 +230,85 @@ def tile_attention_pa_t_kernel(
             nc.gpsimd.tensor_tensor(crossed[:, :, 0, :], high, table(1, 0), ALU.mult)
             nc.gpsimd.tensor_tensor(rot[:, :, 0, :], rot[:, :, 0, :], crossed[:, :, 0, :], ALU.subtract)
             nc.gpsimd.tensor_tensor(rot[:, :, 1, :], rot[:, :, 1, :], crossed[:, :, 1, :], ALU.add)
+            rotated[i] = rot
+
+        def plain_store(i):
+            j, b = PLAIN_TILES[i][0], PLAIN_TILES[i][1]
             for w in range(WEIGHTS):
-                nc.gpsimd.dma_start(out=out_rows[w][:, b, j, :], in_=rot[:, w].rearrange("p h c -> p (h c)"))
+                nc.sync.dma_start(out=out_rows[w][:, b, j, :], in_=rotated[i][:, w].rearrange("p h c -> p (h c)"))
 
         rounds = [(u, w) for u in range(len(UNITS)) for w in range(WEIGHTS)]
         order = [(r, h) for r in range(2) for h in range(2)]
-        operands = {}
-        handed = {}
 
         def project_round(k, wanted=(0, 1)):
             u, w = rounds[k]
-            return {(r, h): project(UNITS[u], w, r, h, operands[u]) for r, h in order if r in wanted}
+            return {(r, h): project(UNITS[u], w, r, h) for r, h in order if r in wanted}
 
         def multiply_round(k, banks):
             u, w = rounds[k]
             return {(r, h): multiply(UNITS[u], r + 2 * h, banks[(r, h)]) for r, h in order}
 
-        def quantised(u, grouped):
-            operands[u] = quantise(UNITS[u], grouped, quant)
-            if u - FIRST_GATE in handed:
-                plain_rotate(u - FIRST_GATE, handed[u - FIRST_GATE], operands[u])
+        def quantised(o, grouped):
+            operands[o] = quantise(OPERANDS[o], grouped, quant)
+            for i in GATED.get(o, ()):
+                plain_rotate(i, operands[o])
 
-        with tc.manual_schedule(engines={mybir.EngineType.PE, mybir.EngineType.Pool}):
-            grouped = new_grouped(UNITS[0], quant)
-            turn_x(UNITS[0], 0, grouped, back, "turned_back")
+        pinned = {mybir.EngineType.PE, mybir.EngineType.Pool, mybir.EngineType.DVE, mybir.EngineType.SP}
+        with tc.manual_schedule(engines=pinned):
+            grouped = new_grouped(OPERANDS[0], quant)
+            turn_x(OPERANDS[0][0], 0, grouped, back, "turned_back")
             quantised(0, grouped)
             turn_tables(UNITS[0][0], flip, "flipped")
             banks = project_round(0)
             prod_of = {}
+            grouped_p = {}
             for k, (u, w) in enumerate(rounds):
                 prod_of[k] = multiply_round(k, banks)
                 if k == 0:
-                    grouped = new_grouped(UNITS[1], quant)
-                    turn_x(UNITS[1], 0, grouped, back, "turned_back")
+                    grouped = new_grouped(OPERANDS[1], quant)
+                    turn_x(OPERANDS[1][0], 0, grouped, back, "turned_back")
                     banks = project_round(1, (0,))
-                    turn_x(UNITS[1], 1, grouped, back, "turned_back")
+                    turn_x(OPERANDS[1][1], 1, grouped, back, "turned_back")
                     quantised(1, grouped)
                     late = project_round(1, (1,))
                     for key in late:
                         banks[key] = late[key]
                     continue
-                more = u + 1 < len(UNITS)
-                second = more and w == 0 and UNITS[u + 1][2] == BATCH
-                if more and w == 0:
-                    grouped = new_grouped(UNITS[u + 1], quant)
-                    turn_x(UNITS[u + 1], 0, grouped, flip, "flipped")
-                    if not second:
-                        quantised(u + 1, grouped)
-                if more and w == 1 and UNITS[u + 1][0] != UNITS[0][0]:
+                coming = u + 1 if w == 0 and u + 1 < len(OPERANDS) else None
+                if coming is not None:
+                    grouped = new_grouped(OPERANDS[coming], quant)
+                    turn_x(OPERANDS[coming][0], 0, grouped, flip, "flipped")
+                if w == 1 and u + 1 < len(UNITS) and UNITS[u + 1][0] != UNITS[0][0]:
                     turn_tables(UNITS[u + 1][0], flip, "flipped")
                 if k == 1:
-                    grouped_p = new_grouped(PLAIN, plain)
+                    grouped_p[0] = new_grouped(PLAIN_OPERANDS[0], plain)
                 for m in ([k - 1] if k > 0 else []) + ([k] if k + 1 == len(rounds) else []):
                     um, wm = rounds[m]
-                    jm, b0, nb = UNITS[um]
+                    jm, b0, nb = UNITS[um][0], UNITS[um][1], UNITS[um][2]
                     out_sb = rows.tile([P, nb, 2, 2, P], F32, name="out_sb")
                     for r in range(2):
-                        join(UNITS[um], [prod_of[m][(r, h)] for h in range(2)], out_sb, r)
-                        if r == 0 and m == k - 1 and second:
-                            turn_x(UNITS[u + 1], 1, grouped, flip, "flipped")
-                            quantised(u + 1, grouped)
+                        early = PROJECTED.get(k) if r == 1 and m == k - 1 else None
+                        join(UNITS[um], [prod_of[m][(r, h)] for h in range(2)], out_sb, r, early)
+                        if r == 0 and m == k - 1 and coming is not None:
+                            turn_x(OPERANDS[coming][1], 1, grouped, flip, "flipped")
                         if k == 1:
-                            turn_x(PLAIN, r, grouped_p, back, "turned_back")
+                            turn_x(PLAIN_OPERANDS[0][r], r, grouped_p[0], back, "turned_back")
+                        if k == 5 and r == 0:
+                            grouped_p[1] = new_grouped(PLAIN_OPERANDS[1], plain)
+                            turn_x(PLAIN_OPERANDS[1][0], 0, grouped_p[1], flip, "flipped")
                     nc.sync.dma_start(
                         out=out_rows[wm][:, b0 : b0 + nb, jm, :],
                         in_=out_sb[:].rearrange("p b h r c -> p b (h r c)"),
                     )
+                if k in STORED:
+                    plain_store(STORED[k])
                 if k == 1:
-                    operand_p = quantise(PLAIN, grouped_p, plain)
-                if w == 1 and 0 <= (k - 3) // 2 < PLAIN[2]:
-                    handed[(k - 3) // 2] = plain_project((k - 3) // 2, operand_p)
+                    plain_operands[0] = quantise(PLAIN_OPERANDS[0], grouped_p[0], plain)
+                if k == 6:
+                    plain_operands[1] = quantise(PLAIN_OPERANDS[1], grouped_p[1], plain)
+                if coming is not None:
+                    quantised(coming, grouped)
+                if PROJECTED.get(k) == len(PLAIN_TILES) - 1:
+                    plain_rotate(PROJECTED[k], None)
                 if k + 1 < len(rounds):
                     banks = project_round(k + 1)

@@ -147,6 +147,7 @@ def tile_attention_pa_t_kernel(
         plain_operands = {}
         handed = {}
         rotated = {}
+        minus_sin = {}
 
         def project(unit, w, r, h):
             j, b0, nb, operand, first = unit
@@ -224,13 +225,22 @@ def tile_attention_pa_t_kernel(
             high = sums_sb[:, 1, :].rearrange("p (w c) -> p w c", w=WEIGHTS)
             rot = plain.tile([P, WEIGHTS, 2, HALF], F32, name="rot")
             crossed = plain.tile([P, WEIGHTS, 2, HALF], F32, name="crossed")
-            nc.gpsimd.tensor_tensor(rot[:, :, 0, :], low, table(0, 0), ALU.mult)
+            nc.gpsimd.tensor_tensor(
+                rot[:].rearrange("p w h c -> p h w c"),
+                sums_sb[:].rearrange("p h (w c) -> p h w c", w=WEIGHTS),
+                raw_of[(j, 0)].rearrange("p (h c) -> p h c", h=2).unsqueeze(2).to_broadcast([P, 2, WEIGHTS, HALF]),
+                ALU.mult,
+            )
             nc.gpsimd.tensor_tensor(crossed[:, :, 1, :], low, table(1, 1), ALU.mult)
-            nc.gpsimd.tensor_tensor(rot[:, :, 1, :], high, table(0, 1), ALU.mult)
-            nc.gpsimd.tensor_tensor(crossed[:, :, 0, :], high, table(1, 0), ALU.mult)
-            nc.gpsimd.tensor_tensor(rot[:, :, 0, :], rot[:, :, 0, :], crossed[:, :, 0, :], ALU.subtract)
-            nc.gpsimd.tensor_tensor(rot[:, :, 1, :], rot[:, :, 1, :], crossed[:, :, 1, :], ALU.add)
+            nc.gpsimd.tensor_tensor(
+                crossed[:, :, 0, :], high, minus_sin[j][:].unsqueeze(1).to_broadcast([P, WEIGHTS, HALF]), ALU.mult
+            )
+            nc.gpsimd.tensor_tensor(rot[:], rot[:], crossed[:], ALU.add)
             rotated[i] = rot
+
+        def negate_sin(j):
+            minus_sin[j] = keep.tile([P, HALF], BF16, name="minus_sin%d" % j)
+            nc.scalar.activation(out=minus_sin[j][:], in_=raw_of[(j, 1)][:, 0:HALF], func=ACT.Copy, scale=-1.0)
 
         def plain_store(i):
             j, b = PLAIN_TILES[i][0], PLAIN_TILES[i][1]
@@ -281,6 +291,7 @@ def tile_attention_pa_t_kernel(
                 if w == 1 and u + 1 < len(UNITS) and UNITS[u + 1][0] != UNITS[0][0]:
                     turn_tables(UNITS[u + 1][0], flip, "flipped")
                 if k == 1:
+                    negate_sin(PLAIN_OPERANDS[0][0][0])
                     grouped_p[0] = new_grouped(PLAIN_OPERANDS[0], plain)
                 for m in ([k - 1] if k > 0 else []) + ([k] if k + 1 == len(rounds) else []):
                     um, wm = rounds[m]
@@ -294,6 +305,7 @@ def tile_attention_pa_t_kernel(
                         if k == 1:
                             turn_x(PLAIN_OPERANDS[0][r], r, grouped_p[0], back, "turned_back")
                         if k == 5 and r == 0:
+                            negate_sin(PLAIN_OPERANDS[1][0][0])
                             grouped_p[1] = new_grouped(PLAIN_OPERANDS[1], plain)
                             turn_x(PLAIN_OPERANDS[1][0], 0, grouped_p[1], flip, "flipped")
                     nc.sync.dma_start(

@@ -56,12 +56,11 @@ def tile_attention_pa_t_kernel(
         tc.tile_pool(name="keep", bufs=1) as keep,
         tc.tile_pool(name="quant", bufs=2) as quant,
         tc.tile_pool(name="prods", bufs=8) as prods,
-        tc.tile_pool(name="rows", bufs=3) as rows,
+        tc.tile_pool(name="rows", bufs=12) as rows,
         tc.tile_pool(name="plain", bufs=2) as plain,
         tc.tile_pool(name="handover", bufs=3) as handover,
-        tc.psum_pool(name="flip", bufs=1) as flip,
         tc.psum_pool(name="sums", bufs=4) as sums,
-        tc.psum_pool(name="back", bufs=3) as back,
+        tc.psum_pool(name="back", bufs=4) as back,
     ):
         tables = {j: keep.tile([P, CHUNKS, 2, P], BF16, name="tables%d" % j) for j in range(ROWS) if j != 1}
         w_words = keep.tile([P, 2, WEIGHTS, 2 * HALF], U8, align_bytes=64)
@@ -176,22 +175,19 @@ def tile_attention_pa_t_kernel(
             )
             return prod
 
-        def join(unit, pair, out_sb, r, before_last=None):
-            for half in range(unit[2] // 2):
-                if before_last is not None and half == unit[2] // 2 - 1:
-                    plain_project(before_last)
-                turned = back.tile([P, 2, 2, P], F32, name="turned_back")
-                for a in range(2):
-                    for h in range(2):
-                        nc.tensor.matmul(
-                            out=turned[:, a, h, :], lhsT=pair[h][:, 0, 2 * half + a, :], rhs=ident[:],
-                            is_transpose=True, start=True, stop=False,
-                        )
-                        nc.tensor.matmul(
-                            out=turned[:, a, h, :], lhsT=pair[1 - h][:, 1, 2 * half + a, :], rhs=ident[:],
-                            is_transpose=True, start=False, stop=True,
-                        )
-                nc.scalar.copy(out=out_sb[:, 2 * half : 2 * half + 2, :, r, :], in_=turned[:])
+        def join(unit, prod, w, b):
+            turned = back.tile([P, CHUNKS, P], F32, name="turned_back")
+            for c in range(CHUNKS):
+                nc.tensor.matmul(
+                    out=turned[:, c, :], lhsT=prod[c][:, 0, b, :], rhs=ident[:], is_transpose=True, start=True, stop=False
+                )
+                nc.tensor.matmul(
+                    out=turned[:, c, :], lhsT=prod[(c + 2) % CHUNKS][:, 1, b, :], rhs=ident[:],
+                    is_transpose=True, start=False, stop=True,
+                )
+            out_sb = rows.tile([P, DIM], F32, name="out_sb")
+            nc.scalar.copy(out=out_sb[:], in_=turned[:].rearrange("p c f -> p (c f)"))
+            nc.sync.dma_start(out=out_rows[w][:, unit[1] + b, unit[0], :], in_=out_sb[:])
 
         def plain_project(i):
             j, b, operand, a = PLAIN_TILES[i]
@@ -268,7 +264,7 @@ def tile_attention_pa_t_kernel(
             grouped = new_grouped(OPERANDS[0], quant)
             turn_x(OPERANDS[0][0], 0, grouped, back, "turned_back")
             quantised(0, grouped)
-            turn_tables(UNITS[0][0], flip, "flipped")
+            turn_tables(UNITS[0][0], back, "turned_back")
             banks = project_round(0)
             prod_of = {}
             grouped_p = {}
@@ -287,31 +283,30 @@ def tile_attention_pa_t_kernel(
                 coming = u + 1 if w == 0 and u + 1 < len(OPERANDS) else None
                 if coming is not None:
                     grouped = new_grouped(OPERANDS[coming], quant)
-                    turn_x(OPERANDS[coming][0], 0, grouped, flip, "flipped")
+                    turn_x(OPERANDS[coming][0], 0, grouped, back, "turned_back")
                 if w == 1 and u + 1 < len(UNITS) and UNITS[u + 1][0] != UNITS[0][0]:
-                    turn_tables(UNITS[u + 1][0], flip, "flipped")
+                    turn_tables(UNITS[u + 1][0], back, "turned_back")
                 if k == 1:
                     negate_sin(PLAIN_OPERANDS[0][0][0])
                     grouped_p[0] = new_grouped(PLAIN_OPERANDS[0], plain)
                 for m in ([k - 1] if k > 0 else []) + ([k] if k + 1 == len(rounds) else []):
                     um, wm = rounds[m]
-                    jm, b0, nb = UNITS[um][0], UNITS[um][1], UNITS[um][2]
-                    out_sb = rows.tile([P, nb, 2, 2, P], F32, name="out_sb")
-                    for r in range(2):
-                        early = PROJECTED.get(k) if r == 1 and m == k - 1 else None
-                        join(UNITS[um], [prod_of[m][(r, h)] for h in range(2)], out_sb, r, early)
-                        if r == 0 and m == k - 1 and coming is not None:
-                            turn_x(OPERANDS[coming][1], 1, grouped, flip, "flipped")
-                        if k == 1:
-                            turn_x(PLAIN_OPERANDS[0][r], r, grouped_p[0], back, "turned_back")
-                        if k == 5 and r == 0:
-                            negate_sin(PLAIN_OPERANDS[1][0][0])
-                            grouped_p[1] = new_grouped(PLAIN_OPERANDS[1], plain)
-                            turn_x(PLAIN_OPERANDS[1][0], 0, grouped_p[1], flip, "flipped")
-                    nc.sync.dma_start(
-                        out=out_rows[wm][:, b0 : b0 + nb, jm, :],
-                        in_=out_sb[:].rearrange("p b h r c -> p b (h r c)"),
-                    )
+                    nb = UNITS[um][2]
+                    for b in range(nb):
+                        if b == nb - 1 and m == k - 1 and k in PROJECTED:
+                            plain_project(PROJECTED[k])
+                        if b == nb // 2:
+                            if m == k - 1 and coming is not None:
+                                turn_x(OPERANDS[coming][1], 1, grouped, back, "turned_back")
+                            if k == 1:
+                                turn_x(PLAIN_OPERANDS[0][0], 0, grouped_p[0], back, "turned_back")
+                            if k == 5:
+                                negate_sin(PLAIN_OPERANDS[1][0][0])
+                                grouped_p[1] = new_grouped(PLAIN_OPERANDS[1], plain)
+                                turn_x(PLAIN_OPERANDS[1][0], 0, grouped_p[1], back, "turned_back")
+                        join(UNITS[um], [prod_of[m][(c % 2, c // 2)] for c in range(CHUNKS)], wm, b)
+                    if k == 1:
+                        turn_x(PLAIN_OPERANDS[0][1], 1, grouped_p[0], back, "turned_back")
                 if k in STORED:
                     plain_store(STORED[k])
                 if k == 1:

@@ -33,16 +33,11 @@ FLOPS = 2 * BATCH * SEQ * DIM * WEIGHTS * DIM
 
 
 def load_weight(nc, words_dram, scales_dram, words, scales, w):
-    nc.sync.dma_start(
-        out=words[:, :, w, :].bitcast(I32),
-        in_=words_dram[0].bitcast(I32).rearrange("p (h c) -> p h c", h=2),
-    )
+    nc.sync.dma_start(out=words[:, w, :].bitcast(I32), in_=words_dram[0].bitcast(I32))
     for quadrant in range(4):
         nc.sync.dma_start(
-            out=scales[32 * quadrant : 32 * quadrant + 4, :, w, :].bitcast(I32),
-            in_=scales_dram[0, 4 * quadrant : 4 * quadrant + 4, :]
-            .bitcast(I32)
-            .rearrange("q (h c) -> q h c", h=2),
+            out=scales[32 * quadrant : 32 * quadrant + 4, w, :].bitcast(I32),
+            in_=scales_dram[0, 4 * quadrant : 4 * quadrant + 4, :].bitcast(I32),
         )
 
 
@@ -63,8 +58,8 @@ def tile_attention_pa_t_kernel(
         tc.psum_pool(name="back", bufs=4) as back,
     ):
         tables = {j: keep.tile([P, CHUNKS, 2, P], BF16, name="tables%d" % j) for j in range(ROWS) if j != 1}
-        w_words = keep.tile([P, 2, WEIGHTS, 2 * HALF], U8, align_bytes=64)
-        w_scales = keep.tile([P, 2, WEIGHTS, HALF], U8, align_bytes=64)
+        w_words = keep.tile([P, WEIGHTS, 2 * DIM], U8, align_bytes=64)
+        w_scales = keep.tile([P, WEIGHTS, DIM], U8, align_bytes=64)
         ident = keep.tile([P, P], F32)
         ident_bf = keep.tile([P, P], BF16)
 
@@ -155,8 +150,8 @@ def tile_attention_pa_t_kernel(
             bank = sums.tile([P, nb * P], F32, name="bank")
             nc.tensor.matmul_mx(
                 out=bank[:],
-                lhsT=w_words[:, h, w, r * 2 * P : (r + 1) * 2 * P].bitcast(FP4X4),
-                lhsT_scale=w_scales[:, h, w, r * P : (r + 1) * P],
+                lhsT=w_words[:, w, (r + 2 * h) * 2 * P : (r + 2 * h + 1) * 2 * P].bitcast(FP4X4),
+                lhsT_scale=w_scales[:, w, (r + 2 * h) * P : (r + 2 * h + 1) * P],
                 rhs=x_codes[:, tokens].bitcast(FP8X4),
                 rhs_scale=x_scales[:, tokens],
                 start=True,
@@ -192,19 +187,19 @@ def tile_attention_pa_t_kernel(
         def plain_project(i):
             j, b, operand, a = PLAIN_TILES[i]
             x_codes, x_scales = plain_operands[operand]
-            sums_sb = handover.tile([P, 2, WEIGHTS * HALF], F32, name="sums_sb")
-            for h in range(2):
-                bank = sums.tile([P, WEIGHTS * HALF], F32, name="bank")
+            sums_sb = handover.tile([P, WEIGHTS, DIM], F32, name="sums_sb")
+            for w in range(WEIGHTS):
+                bank = back.tile([P, DIM], F32, name="turned_back")
                 nc.tensor.matmul_mx(
                     out=bank[:],
                     lhsT=x_codes[:, a * P : (a + 1) * P].bitcast(FP8X4),
                     lhsT_scale=x_scales[:, a * P : (a + 1) * P],
-                    rhs=w_words[:, h].rearrange("p w c -> p (w c)").bitcast(FP4X4),
-                    rhs_scale=w_scales[:, h].rearrange("p w c -> p (w c)"),
+                    rhs=w_words[:, w, :].bitcast(FP4X4),
+                    rhs_scale=w_scales[:, w, :],
                     start=True,
                     stop=True,
                 )
-                nc.scalar.copy(out=sums_sb[:, h, :], in_=bank[:])
+                nc.scalar.copy(out=sums_sb[:, w, :], in_=bank[:])
             handed[i] = sums_sb
 
         def plain_rotate(i, behind):
@@ -217,14 +212,14 @@ def tile_attention_pa_t_kernel(
             if behind is not None:
                 waited = plain.tile([P, 16], U32, name="waited")
                 nc.gpsimd.tensor_copy(out=waited[:], in_=behind[0][:, 0:16])
-            low = sums_sb[:, 0, :].rearrange("p (w c) -> p w c", w=WEIGHTS)
-            high = sums_sb[:, 1, :].rearrange("p (w c) -> p w c", w=WEIGHTS)
+            low = sums_sb[:, :, 0:HALF]
+            high = sums_sb[:, :, HALF:DIM]
             rot = plain.tile([P, WEIGHTS, 2, HALF], F32, name="rot")
             crossed = plain.tile([P, WEIGHTS, 2, HALF], F32, name="crossed")
             nc.gpsimd.tensor_tensor(
-                rot[:].rearrange("p w h c -> p h w c"),
-                sums_sb[:].rearrange("p h (w c) -> p h w c", w=WEIGHTS),
-                raw_of[(j, 0)].rearrange("p (h c) -> p h c", h=2).unsqueeze(2).to_broadcast([P, 2, WEIGHTS, HALF]),
+                rot[:].rearrange("p w h c -> p w (h c)"),
+                sums_sb[:],
+                raw_of[(j, 0)].unsqueeze(1).to_broadcast([P, WEIGHTS, DIM]),
                 ALU.mult,
             )
             nc.gpsimd.tensor_tensor(crossed[:, :, 1, :], low, table(1, 1), ALU.mult)
@@ -293,8 +288,6 @@ def tile_attention_pa_t_kernel(
                     um, wm = rounds[m]
                     nb = UNITS[um][2]
                     for b in range(nb):
-                        if b == nb - 1 and m == k - 1 and k in PROJECTED:
-                            plain_project(PROJECTED[k])
                         if b == nb // 2:
                             if m == k - 1 and coming is not None:
                                 turn_x(OPERANDS[coming][1], 1, grouped, back, "turned_back")
@@ -307,6 +300,8 @@ def tile_attention_pa_t_kernel(
                         join(UNITS[um], [prod_of[m][(c % 2, c // 2)] for c in range(CHUNKS)], wm, b)
                     if k == 1:
                         turn_x(PLAIN_OPERANDS[0][1], 1, grouped_p[0], back, "turned_back")
+                if k in PROJECTED:
+                    plain_project(PROJECTED[k])
                 if k in STORED:
                     plain_store(STORED[k])
                 if k == 1:

@@ -27,7 +27,7 @@ PLAIN_OPERANDS = (((1, 0), (1, 2)), ((7, 0),))
 PLAIN_TILES = tuple((1, b, 0, b) for b in range(BATCH)) + ((7, 0, 1, 0), (7, 1, 1, 1))
 GATED = {2: (0,), 3: (1,), 4: (2,), 5: (3,), 6: (4,)}
 PROJECTED = {2: 0, 3: 1, 5: 2, 7: 3, 9: 4, 11: 5}
-STORED = {4: 0, 6: 1, 8: 2, 10: 3, 13: 4, 15: 5}
+STORED = {4: 0, 6: 1, 8: 2, 10: 3, 13: 4}
 
 FLOPS = 2 * BATCH * SEQ * DIM * WEIGHTS * DIM
 
@@ -49,7 +49,7 @@ def tile_attention_pa_t_kernel(
 
     with (
         tc.tile_pool(name="keep", bufs=1) as keep,
-        tc.tile_pool(name="quant", bufs=2) as quant,
+        tc.tile_pool(name="quant", bufs=3) as quant,
         tc.tile_pool(name="prods", bufs=8) as prods,
         tc.tile_pool(name="rows", bufs=12) as rows,
         tc.tile_pool(name="plain", bufs=2) as plain,
@@ -226,8 +226,9 @@ def tile_attention_pa_t_kernel(
             nc.gpsimd.tensor_tensor(
                 crossed[:, :, 0, :], high, minus_sin[j][:].unsqueeze(1).to_broadcast([P, WEIGHTS, HALF]), ALU.mult
             )
-            nc.gpsimd.tensor_tensor(rot[:], rot[:], crossed[:], ALU.add)
-            rotated[i] = rot
+            if i + 1 < len(PLAIN_TILES):
+                nc.gpsimd.tensor_tensor(rot[:], rot[:], crossed[:], ALU.add)
+            rotated[i] = (rot, crossed)
 
         def negate_sin(j):
             minus_sin[j] = keep.tile([P, HALF], BF16, name="minus_sin%d" % j)
@@ -236,7 +237,7 @@ def tile_attention_pa_t_kernel(
         def plain_store(i):
             j, b = PLAIN_TILES[i][0], PLAIN_TILES[i][1]
             for w in range(WEIGHTS):
-                nc.sync.dma_start(out=out_rows[w][:, b, j, :], in_=rotated[i][:, w].rearrange("p h c -> p (h c)"))
+                nc.sync.dma_start(out=out_rows[w][:, b, j, :], in_=rotated[i][0][:, w].rearrange("p h c -> p (h c)"))
 
         rounds = [(u, w) for u in range(len(UNITS)) for w in range(WEIGHTS)]
         order = [(r, h) for r in range(2) for h in range(2)]
@@ -254,7 +255,7 @@ def tile_attention_pa_t_kernel(
             for i in GATED.get(o, ()):
                 plain_rotate(i, operands[o])
 
-        pinned = {mybir.EngineType.PE, mybir.EngineType.Pool, mybir.EngineType.DVE, mybir.EngineType.SP}
+        pinned = {mybir.EngineType.Activation, mybir.EngineType.PE, mybir.EngineType.Pool, mybir.EngineType.DVE, mybir.EngineType.SP}
         with tc.manual_schedule(engines=pinned):
             grouped = new_grouped(OPERANDS[0], quant)
             turn_x(OPERANDS[0][0], 0, grouped, back, "turned_back")
@@ -264,29 +265,40 @@ def tile_attention_pa_t_kernel(
             prod_of = {}
             grouped_p = {}
             for k, (u, w) in enumerate(rounds):
-                prod_of[k] = multiply_round(k, banks)
+                prod_of[k] = {}
+                for n, (r, h) in enumerate(order):
+                    if k == 2 and n == 2:
+                        plain_operands[0] = quantise(PLAIN_OPERANDS[0], grouped_p[0], plain)
+                    prod_of[k][(r, h)] = multiply(UNITS[u], r + 2 * h, banks[(r, h)])
+                if k == 1:
+                    quantised(1, grouped)
                 if k == 0:
                     grouped = new_grouped(OPERANDS[1], quant)
                     turn_x(OPERANDS[1][0], 0, grouped, back, "turned_back")
                     banks = project_round(1, (0,))
                     turn_x(OPERANDS[1][1], 1, grouped, back, "turned_back")
-                    quantised(1, grouped)
                     late = project_round(1, (1,))
                     for key in late:
                         banks[key] = late[key]
                     continue
                 coming = u + 1 if w == 0 and u + 1 < len(OPERANDS) else None
-                if coming is not None:
+                if coming is not None and coming == 3:
+                    grouped = ahead
+                elif coming is not None:
                     grouped = new_grouped(OPERANDS[coming], quant)
                     turn_x(OPERANDS[coming][0], 0, grouped, back, "turned_back")
                 if w == 1 and u + 1 < len(UNITS) and UNITS[u + 1][0] != UNITS[0][0]:
                     turn_tables(UNITS[u + 1][0], back, "turned_back")
                 if k == 1:
-                    negate_sin(PLAIN_OPERANDS[0][0][0])
                     grouped_p[0] = new_grouped(PLAIN_OPERANDS[0], plain)
                 for m in ([k - 1] if k > 0 else []) + ([k] if k + 1 == len(rounds) else []):
                     um, wm = rounds[m]
                     nb = UNITS[um][2]
+                    if m == k:
+                        rot, crossed = rotated[len(PLAIN_TILES) - 1]
+                        for v in range(WEIGHTS):
+                            nc.vector.tensor_tensor(rot[:, v], rot[:, v], crossed[:, v], ALU.add)
+                        plain_store(len(PLAIN_TILES) - 1)
                     for b in range(nb):
                         if b == nb // 2:
                             if m == k - 1 and coming is not None:
@@ -300,12 +312,14 @@ def tile_attention_pa_t_kernel(
                         join(UNITS[um], [prod_of[m][(c % 2, c // 2)] for c in range(CHUNKS)], wm, b)
                     if k == 1:
                         turn_x(PLAIN_OPERANDS[0][1], 1, grouped_p[0], back, "turned_back")
+                if k == 2:
+                    negate_sin(PLAIN_OPERANDS[0][0][0])
+                    ahead = new_grouped(OPERANDS[3], quant)
+                    turn_x(OPERANDS[3][0], 0, ahead, back, "turned_back")
                 if k in PROJECTED:
                     plain_project(PROJECTED[k])
                 if k in STORED:
                     plain_store(STORED[k])
-                if k == 1:
-                    plain_operands[0] = quantise(PLAIN_OPERANDS[0], grouped_p[0], plain)
                 if k == 6:
                     plain_operands[1] = quantise(PLAIN_OPERANDS[1], grouped_p[1], plain)
                 if coming is not None:

import concourse.mybir as mybir
from concourse.masks import make_identity

F32 = mybir.dt.float32
BF16 = mybir.dt.bfloat16
U8 = mybir.dt.uint8
U32 = mybir.dt.uint32
I32 = mybir.dt.int32
FP8X4 = mybir.dt.float8_e4m3fn_x4
FP4X4 = mybir.dt.float4_e2m1fn_x4
ALU = mybir.AluOpType
ACT = mybir.ActivationFunctionType

P = 128
BATCH = 4
SEQ = 1024
DIM = 512
HALF = DIM // 2
WORDS = DIM // 2
PACK = 4
ROWS = SEQ // P
CHUNKS = DIM // P
WEIGHTS = 2
OPERANDS = (((0, 0),),) + tuple(((j, 0), (j, 2)) for j in range(2, 7)) + (((7, 2), (0, 2)),)
UNITS = ((0, 0, 2, 0, 0),) + tuple((j, 0, BATCH, j - 1, 0) for j in range(2, 7)) + ((7, 2, 2, 6, 0), (0, 2, 2, 6, 1))
PLAIN_OPERANDS = (((1, 0), (1, 2)), ((7, 0),))
PLAIN_TILES = tuple((1, b, 0, b) for b in range(BATCH)) + ((7, 0, 1, 0), (7, 1, 1, 1))
GATED = {2: (0,), 3: (1,), 4: (2,), 5: (3,), 6: (4,)}
PROJECTED = {2: 0, 3: 1, 5: 2, 7: 3, 9: 4, 11: 5}
STORED = {4: 0, 6: 1, 8: 2, 10: 3, 13: 4}

FLOPS = 2 * BATCH * SEQ * DIM * WEIGHTS * DIM


def load_weight(nc, words_dram, scales_dram, words, scales, w):
    nc.sync.dma_start(out=words[:, w, :].bitcast(I32), in_=words_dram[0].bitcast(I32))
    for quadrant in range(4):
        nc.sync.dma_start(
            out=scales[32 * quadrant : 32 * quadrant + 4, w, :].bitcast(I32),
            in_=scales_dram[0, 4 * quadrant : 4 * quadrant + 4, :].bitcast(I32),
        )


def tile_attention_pa_t_kernel(
    tc, x, cos, sin, wq_words, wq_scales, wk_words, wk_scales, out_q, out_k
):
    nc = tc.nc
    out_rows = [o.rearrange("b (p j) d -> p b j d", j=ROWS) for o in (out_q, out_k)]

    with (
        tc.tile_pool(name="keep", bufs=1) as keep,
        tc.tile_pool(name="quant", bufs=3) as quant,
        tc.tile_pool(name="prods", bufs=8) as prods,
        tc.tile_pool(name="rows", bufs=12) as rows,
        tc.tile_pool(name="plain", bufs=2) as plain,
        tc.tile_pool(name="handover", bufs=3) as handover,
        tc.psum_pool(name="sums", bufs=4) as sums,
        tc.psum_pool(name="back", bufs=4) as back,
    ):
        tables = {j: keep.tile([P, CHUNKS, 2, P], BF16, name="tables%d" % j) for j in range(ROWS) if j != 1}
        w_words = keep.tile([P, WEIGHTS, 2 * DIM], U8, align_bytes=64)
        w_scales = keep.tile([P, WEIGHTS, DIM], U8, align_bytes=64)
        ident = keep.tile([P, P], F32)
        ident_bf = keep.tile([P, P], BF16)

        nc.vector.memset(w_scales[:].bitcast(I32), 0)
        make_identity(nc, ident[:])
        make_identity(nc, ident_bf[:])

        x_rows = x.rearrange("b (p j) d -> p b j d", j=ROWS)
        table_rows = [t.rearrange("(p j) d -> p j d", j=ROWS) for t in (cos, sin)]
        x_of = {}
        raw_of = {}

        def load_x(j0, j1, b0, nb):
            piece = keep.tile([P, nb, j1 - j0, DIM], BF16, name="x%d_%d" % (j0, b0))
            nc.sync.dma_start(
                out=piece[:].rearrange("p b j d -> p b (j d)"),
                in_=x_rows[:, b0 : b0 + nb, j0:j1, :].rearrange("p b j d -> p b (j d)"),
            )
            for j in range(j0, j1):
                for b in range(nb):
                    x_of[(j, b0 + b)] = piece[:, b, j - j0, :]

        def load_tables(j0, j1):
            for t in range(2):
                piece = keep.tile([P, j1 - j0, DIM], BF16, name="raw%d_%d" % (t, j0))
                nc.sync.dma_start(out=piece[:], in_=table_rows[t][:, j0:j1, :])
                for j in range(j0, j1):
                    raw_of[(j, t)] = piece[:, j - j0, :]

        load_x(0, 1, 0, 2)
        load_weight(nc, wq_words, wq_scales, w_words, w_scales, 0)
        load_tables(0, 1)
        load_x(2, 3, 0, BATCH)
        load_weight(nc, wk_words, wk_scales, w_words, w_scales, 1)
        load_tables(2, 3)
        load_x(1, 2, 0, BATCH)
        load_tables(1, 2)
        load_x(3, 4, 0, BATCH)
        load_tables(3, 4)
        for j0 in (4, 6):
            load_x(j0, j0 + 2, 0, BATCH)
            load_tables(j0, j0 + 2)
        load_x(0, 1, 2, 2)

        def turn_tables(j, pool, name):
            turned = pool.tile([P, 2, CHUNKS, P], BF16, name=name)
            for t in range(2):
                for c in range(CHUNKS):
                    nc.tensor.transpose(turned[:, t, c, :], raw_of[(j, t)][:, c * P : (c + 1) * P], ident_bf[:])
            nc.scalar.copy(out=tables[j][:, :, 0, :], in_=turned[:, 0])
            nc.scalar.copy(out=tables[j][:, 0:2, 1, :], in_=turned[:, 1, 2:4, :])
            nc.scalar.activation(out=tables[j][:, 2:4, 1, :], in_=turned[:, 1, 0:2, :], func=ACT.Copy, scale=-1.0)

        def turn_x(pair, slot, grouped, pool, name):
            j, b = pair
            flipped = pool.tile([P, 2, 2, P], F32, name=name)
            for a in range(2):
                x_words = x_of[(j, b + a)].bitcast(F32)
                for e in range(2):
                    nc.tensor.transpose(flipped[:, a, e, :], x_words[:, e : WORDS : 2], ident[:])
            nc.scalar.copy(
                out=grouped[:, slot * 2 * P * PACK : (slot + 1) * 2 * P * PACK]
                .bitcast(F32)
                .rearrange("p (a r e) -> p a r e", a=2, e=2),
                in_=flipped[:].rearrange("p a e r -> p a r e"),
            )

        def new_grouped(pairs, pool):
            return pool.tile([P, len(pairs) * 2 * P * PACK], BF16, align_bytes=64, name="grouped")

        def quantise(pairs, grouped, pool):
            tokens = len(pairs) * 2 * P
            x_codes = pool.tile([P, tokens], U32, align_bytes=64, name="x_codes")
            x_scales = pool.tile([P, tokens], U8, align_bytes=64, name="x_scales")
            nc.vector.quantize_mx(out=x_codes[:].bitcast(FP8X4), scales=x_scales[:], in_=grouped[:])
            return x_codes, x_scales

        operands = {}
        plain_operands = {}
        handed = {}
        rotated = {}
        minus_sin = {}

        def project(unit, w, r, h):
            j, b0, nb, operand, first = unit
            x_codes, x_scales = operands[operand]
            tokens = slice(first * 2 * P, first * 2 * P + nb * P)
            bank = sums.tile([P, nb * P], F32, name="bank")
            nc.tensor.matmul_mx(
                out=bank[:],
                lhsT=w_words[:, w, (r + 2 * h) * 2 * P : (r + 2 * h + 1) * 2 * P].bitcast(FP4X4),
                lhsT_scale=w_scales[:, w, (r + 2 * h) * P : (r + 2 * h + 1) * P],
                rhs=x_codes[:, tokens].bitcast(FP8X4),
                rhs_scale=x_scales[:, tokens],
                start=True,
                stop=True,
            )
            return bank

        def multiply(unit, c, bank):
            j, nb = unit[0], unit[2]
            prod = prods.tile([P, 2, nb, P], F32, name="prod")
            nc.vector.tensor_tensor(
                prod[:],
                bank[:].rearrange("p (b r) -> p b r", b=nb).unsqueeze(1).to_broadcast([P, 2, nb, P]),
                tables[j][:, c, :, :].unsqueeze(2).to_broadcast([P, 2, nb, P]),
                ALU.mult,
            )
            return prod

        def join(unit, prod, w, b):
            turned = back.tile([P, CHUNKS, P], F32, name="turned_back")
            for c in range(CHUNKS):
                nc.tensor.matmul(
                    out=turned[:, c, :], lhsT=prod[c][:, 0, b, :], rhs=ident[:], is_transpose=True, start=True, stop=False
                )
                nc.tensor.matmul(
                    out=turned[:, c, :], lhsT=prod[(c + 2) % CHUNKS][:, 1, b, :], rhs=ident[:],
                    is_transpose=True, start=False, stop=True,
                )
            out_sb = rows.tile([P, DIM], F32, name="out_sb")
            nc.scalar.copy(out=out_sb[:], in_=turned[:].rearrange("p c f -> p (c f)"))
            nc.sync.dma_start(out=out_rows[w][:, unit[1] + b, unit[0], :], in_=out_sb[:])

        def plain_project(i):
            j, b, operand, a = PLAIN_TILES[i]
            x_codes, x_scales = plain_operands[operand]
            sums_sb = handover.tile([P, WEIGHTS, DIM], F32, name="sums_sb")
            for w in range(WEIGHTS):
                bank = back.tile([P, DIM], F32, name="turned_back")
                nc.tensor.matmul_mx(
                    out=bank[:],
                    lhsT=x_codes[:, a * P : (a + 1) * P].bitcast(FP8X4),
                    lhsT_scale=x_scales[:, a * P : (a + 1) * P],
                    rhs=w_words[:, w, :].bitcast(FP4X4),
                    rhs_scale=w_scales[:, w, :],
                    start=True,
                    stop=True,
                )
                nc.scalar.copy(out=sums_sb[:, w, :], in_=bank[:])
            handed[i] = sums_sb

        def plain_rotate(i, behind):
            j, b = PLAIN_TILES[i][0], PLAIN_TILES[i][1]
            sums_sb = handed[i]

            def table(t, h):
                return raw_of[(j, t)][:, h * HALF : (h + 1) * HALF].unsqueeze(1).to_broadcast([P, WEIGHTS, HALF])

            if behind is not None:
                waited = plain.tile([P, 16], U32, name="waited")
                nc.gpsimd.tensor_copy(out=waited[:], in_=behind[0][:, 0:16])
            low = sums_sb[:, :, 0:HALF]
            high = sums_sb[:, :, HALF:DIM]
            rot = plain.tile([P, WEIGHTS, 2, HALF], F32, name="rot")
            crossed = plain.tile([P, WEIGHTS, 2, HALF], F32, name="crossed")
            nc.gpsimd.tensor_tensor(
                rot[:].rearrange("p w h c -> p w (h c)"),
                sums_sb[:],
                raw_of[(j, 0)].unsqueeze(1).to_broadcast([P, WEIGHTS, DIM]),
                ALU.mult,
            )
            nc.gpsimd.tensor_tensor(crossed[:, :, 1, :], low, table(1, 1), ALU.mult)
            nc.gpsimd.tensor_tensor(
                crossed[:, :, 0, :], high, minus_sin[j][:].unsqueeze(1).to_broadcast([P, WEIGHTS, HALF]), ALU.mult
            )
            if i + 1 < len(PLAIN_TILES):
                nc.gpsimd.tensor_tensor(rot[:], rot[:], crossed[:], ALU.add)
            rotated[i] = (rot, crossed)

        def negate_sin(j):
            minus_sin[j] = keep.tile([P, HALF], BF16, name="minus_sin%d" % j)
            nc.scalar.activation(out=minus_sin[j][:], in_=raw_of[(j, 1)][:, 0:HALF], func=ACT.Copy, scale=-1.0)

        def plain_store(i):
            j, b = PLAIN_TILES[i][0], PLAIN_TILES[i][1]
            for w in range(WEIGHTS):
                nc.sync.dma_start(out=out_rows[w][:, b, j, :], in_=rotated[i][0][:, w].rearrange("p h c -> p (h c)"))

        rounds = [(u, w) for u in range(len(UNITS)) for w in range(WEIGHTS)]
        order = [(r, h) for r in range(2) for h in range(2)]

        def project_round(k, wanted=(0, 1)):
            u, w = rounds[k]
            return {(r, h): project(UNITS[u], w, r, h) for r, h in order if r in wanted}

        def multiply_round(k, banks):
            u, w = rounds[k]
            return {(r, h): multiply(UNITS[u], r + 2 * h, banks[(r, h)]) for r, h in order}

        def quantised(o, grouped):
            operands[o] = quantise(OPERANDS[o], grouped, quant)
            for i in GATED.get(o, ()):
                plain_rotate(i, operands[o])

        pinned = {mybir.EngineType.Activation, mybir.EngineType.PE, mybir.EngineType.Pool, mybir.EngineType.DVE, mybir.EngineType.SP}
        with tc.manual_schedule(engines=pinned):
            grouped = new_grouped(OPERANDS[0], quant)
            turn_x(OPERANDS[0][0], 0, grouped, back, "turned_back")
            quantised(0, grouped)
            turn_tables(UNITS[0][0], back, "turned_back")
            banks = project_round(0)
            prod_of = {}
            grouped_p = {}
            for k, (u, w) in enumerate(rounds):
                prod_of[k] = {}
                for n, (r, h) in enumerate(order):
                    if k == 2 and n == 2:
                        plain_operands[0] = quantise(PLAIN_OPERANDS[0], grouped_p[0], plain)
                    prod_of[k][(r, h)] = multiply(UNITS[u], r + 2 * h, banks[(r, h)])
                if k == 1:
                    quantised(1, grouped)
                if k == 0:
                    grouped = new_grouped(OPERANDS[1], quant)
                    turn_x(OPERANDS[1][0], 0, grouped, back, "turned_back")
                    banks = project_round(1, (0,))
                    turn_x(OPERANDS[1][1], 1, grouped, back, "turned_back")
                    late = project_round(1, (1,))
                    for key in late:
                        banks[key] = late[key]
                    continue
                coming = u + 1 if w == 0 and u + 1 < len(OPERANDS) else None
                if coming is not None and coming == 3:
                    grouped = ahead
                elif coming is not None:
                    grouped = new_grouped(OPERANDS[coming], quant)
                    turn_x(OPERANDS[coming][0], 0, grouped, back, "turned_back")
                if w == 1 and u + 1 < len(UNITS) and UNITS[u + 1][0] != UNITS[0][0]:
                    turn_tables(UNITS[u + 1][0], back, "turned_back")
                if k == 1:
                    grouped_p[0] = new_grouped(PLAIN_OPERANDS[0], plain)
                for m in ([k - 1] if k > 0 else []) + ([k] if k + 1 == len(rounds) else []):
                    um, wm = rounds[m]
                    nb = UNITS[um][2]
                    if m == k:
                        rot, crossed = rotated[len(PLAIN_TILES) - 1]
                        for v in range(WEIGHTS):
                            nc.vector.tensor_tensor(rot[:, v], rot[:, v], crossed[:, v], ALU.add)
                        plain_store(len(PLAIN_TILES) - 1)
                    for b in range(nb):
                        if b == nb // 2:
                            if m == k - 1 and coming is not None:
                                turn_x(OPERANDS[coming][1], 1, grouped, back, "turned_back")
                            if k == 1:
                                turn_x(PLAIN_OPERANDS[0][0], 0, grouped_p[0], back, "turned_back")
                            if k == 5:
                                negate_sin(PLAIN_OPERANDS[1][0][0])
                                grouped_p[1] = new_grouped(PLAIN_OPERANDS[1], plain)
                                turn_x(PLAIN_OPERANDS[1][0], 0, grouped_p[1], back, "turned_back")
                        join(UNITS[um], [prod_of[m][(c % 2, c // 2)] for c in range(CHUNKS)], wm, b)
                    if k == 1:
                        turn_x(PLAIN_OPERANDS[0][1], 1, grouped_p[0], back, "turned_back")
                if k == 2:
                    negate_sin(PLAIN_OPERANDS[0][0][0])
                    ahead = new_grouped(OPERANDS[3], quant)
                    turn_x(OPERANDS[3][0], 0, ahead, back, "turned_back")
                if k in PROJECTED:
                    plain_project(PROJECTED[k])
                if k in STORED:
                    plain_store(STORED[k])
                if k == 6:
                    plain_operands[1] = quantise(PLAIN_OPERANDS[1], grouped_p[1], plain)
                if coming is not None:
                    quantised(coming, grouped)
                if PROJECTED.get(k) == len(PLAIN_TILES) - 1:
                    plain_rotate(PROJECTED[k], None)
                if k + 1 < len(rounds):
                    banks = project_round(k + 1)
